import numpy as np
import ml_dtypes


def mxq(x, axis, fmt="e4m3"):
    dtype, down = {"e4m3": (ml_dtypes.float8_e4m3fn, 7), "e5m2": (ml_dtypes.float8_e5m2, 14)}[fmt]
    v = np.moveaxis(np.asarray(x, np.float32).astype(ml_dtypes.bfloat16).astype(np.float64), axis, -1)
    blocks = v.reshape(v.shape[:-1] + (-1, 32))
    amax = np.abs(blocks).max(-1, keepdims=True)
    byte = np.maximum(np.where(amax > 0, np.frexp(amax)[1] - 1 + 127, 0) - down, 1)
    scale = np.exp2(byte - 127.0)
    codes = (blocks / scale).astype(np.float32).astype(dtype).astype(np.float64)
    return np.moveaxis((codes * scale).reshape(v.shape), -1, axis)


WIDE = False


def mx_kscale(k):
    if not WIDE:
        return np.ones(k)
    levels = np.array([10, -10, 5, -5, 0])
    a = np.random.permutation(np.resize(levels, k // 512 * 4)).reshape(k // 512, 4)
    idx = np.arange(k)
    return np.exp2(a[idx // 512, idx % 128 // 32])


BF16 = ml_dtypes.bfloat16


def bf(x):
    return np.asarray(x, np.float32).astype(BF16)


def f64(x):
    return np.asarray(x).astype(np.float64)


B, ND, NS, D = 2, 512, 512, 512
NUM_ITERS = 5
REG = 0.1
EPS = 1e-12


def l2_normalize(v):
    n = np.sqrt(np.sum(v * v, axis=-1, keepdims=True))
    return v / np.maximum(n, EPS)


def logsumexp(v, axis):
    m = np.max(v, axis=axis, keepdims=True)
    return m + np.log(np.sum(np.exp(v - m), axis=axis, keepdims=True))


def setup_inputs():
    s, t = mx_kscale(D), mx_kscale(D)
    c0 = np.random.standard_normal((B, 1, D))
    c1 = np.random.standard_normal((B, 1, D))
    gd = np.random.random((B, ND, 1)) < 0.7
    gs = np.random.random((B, NS, 1)) < 0.3
    drone = np.random.standard_normal((B, ND, D)) + 1.44 * np.where(gd, c0, c1)
    sat = np.random.standard_normal((B, NS, D)) + 1.44 * np.where(gs, c0, c1)
    w0 = np.random.standard_normal((D, D))
    wq = (w0 + 0.5 * np.random.standard_normal((D, D))) * 0.9 / np.sqrt(D)
    wk = (w0 + 0.5 * np.random.standard_normal((D, D))) * 0.9 / np.sqrt(D)
    return {"drone_tokens": bf(drone * s), "sat_tokens": bf(sat * t),
            "Wq": bf(wq / s), "bq": bf(np.random.standard_normal(D) * 0.5),
            "Wk": bf(wk / t), "bk": bf(np.random.standard_normal(D) * 0.5)}


def reference(drone_tokens, sat_tokens, Wq, bq, Wk, bk):
    q = l2_normalize((mxq(f64(drone_tokens), 2, "e4m3") @ mxq(f64(Wq), 1, "e4m3").T) + f64(bq))
    k = l2_normalize((mxq(f64(sat_tokens), 2, "e4m3") @ mxq(f64(Wk), 1, "e4m3").T) + f64(bk))
    cost = 1.0 - (mxq(q, 2, "e4m3") @ mxq(k, 2, "e4m3").transpose(0, 2, 1))
    M = -cost / REG
    for _ in range(NUM_ITERS):
        M = M - logsumexp(M, 2)
        M = M - logsumexp(M, 1)
    transport_plan = np.exp(M)
    ot_cost = np.mean(np.sum(transport_plan * cost, axis=(1, 2)))
    return transport_plan, ot_cost

@@ -1,0 +1,296 @@
+from contextlib import ExitStack
+
+import concourse.mybir as mybir
+from concourse.masks import make_identity
+
+F32 = mybir.dt.float32
+BF16 = mybir.dt.bfloat16
+U32 = mybir.dt.uint32
+U8 = mybir.dt.uint8
+FP8X4 = mybir.dt.float8_e4m3fn_x4
+ACT = mybir.ActivationFunctionType
+ALU = mybir.AluOpType
+AX = mybir.AxisListType
+
+P = 128
+D = 512
+NT = 4
+B = 2
+ITERS = 5
+FLOPS = 2 * 2 * (B * 512) * D * D + 2 * B * 512 * 512 * D
+
+
+def tile_sinkhornot_kernel(tc, drone_tokens, sat_tokens, Wq, bq, Wk, bk, out_0, out_1):
+    nc = tc.nc
+    with ExitStack() as ctx:
+        const = ctx.enter_context(tc.tile_pool(name="const", bufs=1))
+        keep = ctx.enter_context(tc.tile_pool(name="keep", bufs=1))
+        grp = ctx.enter_context(tc.tile_pool(name="grp", bufs=3))
+        ypool = ctx.enter_context(tc.tile_pool(name="ypool", bufs=8))
+        junk = ctx.enter_context(tc.tile_pool(name="junk", bufs=2))
+        vec = ctx.enter_context(tc.tile_pool(name="vec", bufs=3))
+        outp = ctx.enter_context(tc.tile_pool(name="outp", bufs=4))
+        ps_tp = ctx.enter_context(tc.psum_pool(name="ps_tp", bufs=2))
+        ps_mm = ctx.enter_context(tc.psum_pool(name="ps_mm", bufs=3))
+        ps_qt = ctx.enter_context(tc.psum_pool(name="ps_qt", bufs=3))
+
+        counter = [0]
+
+        def evac(out, in_):
+            counter[0] += 1
+            if counter[0] % 2 == 0:
+                nc.vector.tensor_copy(out=out, in_=in_)
+            else:
+                nc.scalar.copy(out=out, in_=in_)
+
+        ident_f = const.tile([P, P], F32, name="ident_f")
+        make_identity(nc, ident_f[:])
+        ident_b = const.tile([P, P], BF16, name="ident_b")
+        make_identity(nc, ident_b[:])
+        ones_b = const.tile([P, P], BF16, name="ones_b")
+        nc.vector.memset(ones_b[:], 1.0)
+        ones_f = const.tile([P, P], F32, name="ones_f")
+        nc.vector.memset(ones_f[:], 1.0)
+        neg10 = const.tile([P, 1], F32, name="neg10")
+        nc.vector.memset(neg10[:], -10.0)
+
+        brows = []
+        for i, bvec in enumerate((bq, bk)):
+            brow = const.tile([P, D], BF16, name="brow%d" % i)
+            nc.vector.memset(brow[:], 0.0)
+            nc.scalar.dma_start(out=brow[0:1, :], in_=bvec.rearrange("(o f) -> o f", o=1))
+            brows.append(brow)
+
+        def load(name, view):
+            raw = keep.tile([P, NT * D], BF16, name=name)
+            nc.sync.dma_start(out=raw[:].rearrange("p (n k) -> p n k", n=NT), in_=view)
+            return raw
+
+        raw_wq = load("raw_wq", Wq.rearrange("(p n) k -> p n k", n=NT))
+        raw_d0 = load("raw_d0", drone_tokens[0].rearrange("(p n) k -> p n k", n=NT))
+        raw_wk = load("raw_wk", Wk.rearrange("(p n) k -> p n k", n=NT))
+        raw_s0 = load("raw_s0", sat_tokens[0].rearrange("(n p) k -> p n k", p=P))
+        raw_d1 = load("raw_d1", drone_tokens[1].rearrange("(p n) k -> p n k", n=NT))
+        raw_s1 = load("raw_s1", sat_tokens[1].rearrange("(n p) k -> p n k", p=P))
+
+        def mx_tiles(name):
+            codes = keep.tile([P, D], U32, name="c_" + name, align_bytes=64)
+            scales = keep.tile([P, D], U8, name="s_" + name, align_bytes=64)
+            return codes, scales
+
+        def quantise(grouped, cs):
+            nc.vector.quantize_mx(out=cs[0][:].bitcast(FP8X4), scales=cs[1][:], in_=grouped[:])
+
+        def pack_input(raw, name):
+            cs = mx_tiles(name)
+            words = raw[:].bitcast(F32)
+            grouped = grp.tile([P, NT * P * 4], BF16, tag="grouped", align_bytes=64)
+            gw = grouped[:].bitcast(F32).rearrange("p (h r w u) -> p h r w u", h=2, r=2, w=P, u=2)
+            for h in range(2):
+                xt = ps_tp.tile([P, 2, 2, P], F32, tag="tp")
+                for r in range(2):
+                    for u in range(2):
+                        col = (2 * h + r) * 256 + u * P
+                        nc.tensor.transpose(xt[:, r, u, :], words[:, col:col + P], ident_f[:])
+                evac(gw[:, h], xt[:].rearrange("p r u w -> p r w u"))
+            quantise(grouped, cs)
+            return cs
+
+        def bias_tile(i):
+            ps = ps_mm.tile([P, D], F32, tag="mm")
+            nc.tensor.matmul(out=ps[:], lhsT=ones_b[:], rhs=brows[i][:], start=True, stop=True)
+            bias_sb = const.tile([P, D], F32, name="bias%d" % i)
+            nc.vector.tensor_copy(
+                out=bias_sb[:].rearrange("p (n q) -> p n q", n=NT),
+                in_=ps[:].rearrange("p (q n) -> p n q", n=NT),
+            )
+            return bias_sb
+
+        def project(tok, w, bias_sb, g):
+            ss = keep.tile([P, NT], F32, name="ss" + g)
+            ys = []
+            for n in range(NT):
+                z = ps_mm.tile([P, D], F32, tag="mm")
+                nc.tensor.matmul_mx(
+                    out=z[:],
+                    lhsT=tok[0][:, n * P:(n + 1) * P].bitcast(FP8X4),
+                    lhsT_scale=tok[1][:, n * P:(n + 1) * P],
+                    rhs=w[0][:].bitcast(FP8X4),
+                    rhs_scale=w[1][:],
+                    start=True,
+                    stop=True,
+                )
+                y = ypool.tile([P, D], F32, tag="y")
+                nc.vector.tensor_tensor(out=y[:], in0=z[:], in1=bias_sb[:], op=ALU.add)
+                sq = junk.tile([P, D], BF16, tag="sq")
+                nc.scalar.activation(out=sq[:], in_=y[:], func=ACT.Square, accum_out=ss[:, n:n + 1])
+                ys.append(y)
+            ssc = keep.tile([P, NT], F32, name="ssc" + g)
+            nc.vector.tensor_scalar_max(out=ssc[:], in0=ss[:], scalar1=1e-24)
+            nrm = keep.tile([P, NT], F32, name="nrm" + g)
+            nc.scalar.activation(out=nrm[:], in_=ssc[:], func=ACT.Sqrt)
+            rn = keep.tile([P, NT], F32, name="rn" + g)
+            nc.vector.reciprocal(out=rn[:], in_=nrm[:])
+            qbs = []
+            for n in range(NT):
+                qb = keep.tile([P, D], BF16, name="qb%s_%d" % (g, n))
+                nc.gpsimd.tensor_scalar(
+                    out=qb[:], in0=ys[n][:], scalar1=rn[:, n:n + 1], scalar2=0.0, op0=ALU.mult, op1=ALU.add
+                )
+                qbs.append(qb)
+            return qbs
+
+        def pack_features(qbs, name):
+            cs = mx_tiles(name)
+            grouped = grp.tile([P, NT * P * 4], BF16, tag="grouped", align_bytes=64)
+            gv = grouped[:].rearrange("p (h r w t) -> p h r w t", h=2, r=2, w=P, t=4)
+            for h in range(2):
+                qt = ps_qt.tile([P, 2, NT, P], BF16, tag="qt")
+                for r in range(2):
+                    for t in range(NT):
+                        nc.tensor.transpose(qt[:, r, t, :], qbs[2 * h + r][:, t * P:(t + 1) * P], ident_b[:])
+                evac(gv[:, h], qt[:].rearrange("p r t w -> p r w t"))
+            quantise(grouped, cs)
+            return cs
+
+        cwq = pack_input(raw_wq, "wq")
+        cd0 = pack_input(raw_d0, "d0")
+        bias_q = bias_tile(0)
+        q0 = project(cd0, cwq, bias_q, "d0")
+        cwk = pack_input(raw_wk, "wk")
+        cs0 = pack_input(raw_s0, "s0")
+        bias_k = bias_tile(1)
+        k0 = project(cs0, cwk, bias_k, "s0")
+        cq0 = pack_features(q0, "q0")
+        cd1 = pack_input(raw_d1, "d1")
+        q1 = project(cd1, cwq, bias_q, "d1")
+        ck0 = pack_features(k0, "k0")
+        cs1 = pack_input(raw_s1, "s1")
+        k1 = project(cs1, cwk, bias_k, "s1")
+        cq1 = pack_features(q1, "q1")
+        ck1 = pack_features(k1, "k1")
+        cq = [cq0, cq1]
+        ck = [ck0, ck1]
+
+        E = [[], []]
+        C = [[], []]
+        KH = [[], []]
+        KL = [[], []]
+        rsum = []
+        for b in range(B):
+            r1 = keep.tile([P, NT], F32, name="r1_%d" % b)
+            rsum.append(r1)
+            for n in range(NT):
+                z = ps_mm.tile([P, D], F32, tag="mm")
+                nc.tensor.matmul_mx(
+                    out=z[:],
+                    lhsT=cq[b][0][:, n * P:(n + 1) * P].bitcast(FP8X4),
+                    lhsT_scale=cq[b][1][:, n * P:(n + 1) * P],
+                    rhs=ck[b][0][:].bitcast(FP8X4),
+                    rhs_scale=ck[b][1][:],
+                    start=True,
+                    stop=True,
+                )
+                e = keep.tile([P, D], F32, name="e%d_%d" % (b, n))
+                nc.scalar.activation(
+                    out=e[:], in_=z[:], func=ACT.Exp, scale=10.0, bias=neg10[:], accum_out=r1[:, n:n + 1]
+                )
+                c = keep.tile([P, D], F32, name="c%d_%d" % (b, n))
+                nc.vector.tensor_scalar(out=c[:], in0=z[:], scalar1=-1.0, scalar2=1.0, op0=ALU.mult, op1=ALU.add)
+                kh = keep.tile([P, D], BF16, name="kh%d_%d" % (b, n))
+                nc.gpsimd.tensor_scalar(out=kh[:], in0=e[:], scalar1=1.0, scalar2=0.0, op0=ALU.mult, op1=ALU.add)
+                kl = keep.tile([P, D], BF16, name="kl%d_%d" % (b, n))
+                nc.gpsimd.tensor_tensor(out=kl[:], in0=e[:], in1=kh[:], op=ALU.subtract)
+                E[b].append(e)
+                C[b].append(c)
+                KH[b].append(kh)
+                KL[b].append(kl)
+
+        def transpose_kernel(b):
+            kts = []
+            for m in range(NT):
+                kt_ps = ps_qt.tile([P, 2, NT, P], BF16, tag="qt")
+                for s, src in enumerate((KH[b], KL[b])):
+                    for n in range(NT):
+                        nc.tensor.transpose(kt_ps[:, s, n, :], src[n][:, m * P:(m + 1) * P], ident_b[:])
+                kt = keep.tile([P, 2, NT, P], BF16, name="kt%d_%d" % (b, m))
+                evac(kt[:], kt_ps[:])
+                kts.append(kt)
+            return kts
+
+        def invert(s, b):
+            v = vec.tile([P, NT], F32, tag="v%d" % b)
+            nc.vector.reciprocal(out=v[:], in_=s)
+            hl = vec.tile([P, NT, 2], BF16, tag="hl%d" % b)
+            nc.vector.tensor_copy(out=hl[:, :, 0], in_=v[:])
+            nc.vector.tensor_tensor(out=hl[:, :, 1], in0=v[:], in1=hl[:, :, 0], op=ALU.subtract)
+            return v, hl
+
+        def matvec(b, stationary, hl):
+            acc = ps_tp.tile([P, NT, 2], F32, tag="tp")
+            for m in range(NT):
+                for c in range(NT):
+                    for s in range(2):
+                        nc.tensor.matmul(
+                            out=acc[:, m, :],
+                            lhsT=stationary(s, c, m),
+                            rhs=hl[:, c, :],
+                            start=(c == 0 and s == 0),
+                            stop=(c == NT - 1 and s == 1),
+                        )
+            tot = vec.tile([P, NT], F32, tag="tot%d" % b)
+            nc.vector.tensor_reduce(out=tot[:], in_=acc[:], axis=AX.X, op=ALU.add)
+            return invert(tot[:], b)
+
+        KT = [None, None]
+        av = [None, None]
+        bv = [None, None]
+        for b in range(B):
+            av[b] = invert(rsum[b][:], b)
+
+        def col_stat(b):
+            return lambda s, c, m: (KH[b], KL[b])[s][c][:, m * P:(m + 1) * P]
+
+        def row_stat(b):
+            return lambda s, c, m: KT[b][c][:, s, m, :]
+
+        for it in range(ITERS):
+            if it > 0:
+                for b in range(B):
+                    av[b] = matvec(b, row_stat(b), bv[b][1])
+            for b in range(B):
+                bv[b] = matvec(b, col_stat(b), av[b][1])
+                if it == 0:
+                    KT[b] = transpose_kernel(b)
+
+        otp = keep.tile([P, B * NT], F32, name="otp")
+        for b in range(B):
+            bb = ps_mm.tile([P, D], F32, tag="mm")
+            for m in range(NT):
+                nc.tensor.transpose(
+                    bb[:, m * P:(m + 1) * P], bv[b][0][:, m:m + 1].to_broadcast([P, P]), ident_f[:]
+                )
+            dst = out_0[b].rearrange("(p n) j -> p n j", n=NT)
+            for n in range(NT):
+                ka = keep.tile([P, D], F32, name="ka%d_%d" % (b, n))
+                nc.scalar.activation(out=ka[:], in_=E[b][n][:], func=ACT.Copy, scale=av[b][0][:, n:n + 1])
+                plan = outp.tile([P, D], F32, tag="plan")
+                nc.vector.tensor_tensor(out=plan[:], in0=ka[:], in1=bb[:], op=ALU.mult)
+                nc.sync.dma_start(out=dst[:, n, :], in_=plan[:])
+                pc = junk.tile([P, D], F32, tag="pc")
+                nc.vector.scalar_tensor_tensor(
+                    out=pc[:], in0=plan[:], scalar=1.0, in1=C[b][n][:], op0=ALU.mult, op1=ALU.mult,
+                    accum_out=otp[:, b * NT + n:b * NT + n + 1],
+                )
+
+        tot2 = keep.tile([P, 2], F32, name="tot2")
+        nc.vector.memset(tot2[:], 0.0)
+        nc.vector.tensor_reduce(out=tot2[:, 0:1], in_=otp[:], axis=AX.X, op=ALU.add)
+        fin = ps_tp.tile([P, 2], F32, tag="tp")
+        nc.tensor.matmul(out=fin[:], lhsT=ones_f[:], rhs=tot2[:], start=True, stop=True)
+        res = keep.tile([P, 1], F32, name="res")
+        nc.scalar.mul(out=res[:], in_=fin[:, 0:1], mul=1.0 / B)
+        o1 = out_1
+        while len(o1.shape) < 2:
+            o1 = o1.unsqueeze(0)
+        nc.sync.dma_start(out=o1, in_=res[0:1, 0:1])

@@ -17,42 +17,39 @@ D = 512
 NT = 4
 B = 2
 ITERS = 5
+QI_OFF = 1.3
+IE_ENG = {"wq":"SV","d0":"SV","wk":"SS","s0":"SS","d1":"VS","s1":"SS"}
+L_ENG = ("VGVG","VGVV")
+CH = (5.5,7.5,10,12.3)
+CS = (19.3,21.5)
+SCALE_ENG = ("GVSG","GVGG","SGGS","GVVG")
+FE_ENG = ("SV","SS","SS","SV")
+H_ENG = ("VSSS","SVSS")
+OFF = {"A":0.4,"S":1.1,"R":3.2,"C":3.9,"dC":0.6,"FT":5,"dF":1.2,"FE":6.1,"QF":8,"X":0.6,"H":1.3,"G":1.7,"L":1.8,"ET":2.6,"EE":3.9}
+DUM = {"in": 0, "ft": 0, "et": 0, "sk": (0, 0)}
 FLOPS = 2 * 2 * (B * 512) * D * D + 2 * B * 512 * 512 * D
 
 
 def tile_sinkhornot_kernel(tc, drone_tokens, sat_tokens, Wq, bq, Wk, bk, out_0, out_1):
     nc = tc.nc
     with ExitStack() as ctx:
+        ctx.enter_context(tc.manual_schedule())
         const = ctx.enter_context(tc.tile_pool(name="const", bufs=1))
         keep = ctx.enter_context(tc.tile_pool(name="keep", bufs=1))
         grp = ctx.enter_context(tc.tile_pool(name="grp", bufs=3))
-        ypool = ctx.enter_context(tc.tile_pool(name="ypool", bufs=8))
+        ypool = ctx.enter_context(tc.tile_pool(name="ypool", bufs=12))
+        qpool = ctx.enter_context(tc.tile_pool(name="qpool", bufs=12))
         junk = ctx.enter_context(tc.tile_pool(name="junk", bufs=2))
         vec = ctx.enter_context(tc.tile_pool(name="vec", bufs=3))
         outp = ctx.enter_context(tc.tile_pool(name="outp", bufs=4))
-        ps_tp = ctx.enter_context(tc.psum_pool(name="ps_tp", bufs=2))
-        ps_mm = ctx.enter_context(tc.psum_pool(name="ps_mm", bufs=3))
-        ps_qt = ctx.enter_context(tc.psum_pool(name="ps_qt", bufs=3))
+        ps_f = ctx.enter_context(tc.psum_pool(name="ps_f", bufs=6))
+        ps_b = ctx.enter_context(tc.psum_pool(name="ps_b", bufs=2))
 
-        counter = [0]
-
-        def evac(out, in_):
-            counter[0] += 1
-            if counter[0] % 2 == 0:
+        def copy_on(eng, out, in_):
+            if eng == "V":
                 nc.vector.tensor_copy(out=out, in_=in_)
             else:
                 nc.scalar.copy(out=out, in_=in_)
-
-        ident_f = const.tile([P, P], F32, name="ident_f")
-        make_identity(nc, ident_f[:])
-        ident_b = const.tile([P, P], BF16, name="ident_b")
-        make_identity(nc, ident_b[:])
-        ones_b = const.tile([P, P], BF16, name="ones_b")
-        nc.vector.memset(ones_b[:], 1.0)
-        ones_f = const.tile([P, P], F32, name="ones_f")
-        nc.vector.memset(ones_f[:], 1.0)
-        neg10 = const.tile([P, 1], F32, name="neg10")
-        nc.vector.memset(neg10[:], -10.0)
 
         brows = []
         for i, bvec in enumerate((bq, bk)):
@@ -66,168 +63,223 @@ def tile_sinkhornot_kernel(tc, drone_tokens, sat_tokens, Wq, bq, Wk, bk, out_0, 
             nc.sync.dma_start(out=raw[:].rearrange("p (n k) -> p n k", n=NT), in_=view)
             return raw
 
-        raw_wq = load("raw_wq", Wq.rearrange("(p n) k -> p n k", n=NT))
-        raw_d0 = load("raw_d0", drone_tokens[0].rearrange("(p n) k -> p n k", n=NT))
-        raw_wk = load("raw_wk", Wk.rearrange("(p n) k -> p n k", n=NT))
-        raw_s0 = load("raw_s0", sat_tokens[0].rearrange("(n p) k -> p n k", p=P))
-        raw_d1 = load("raw_d1", drone_tokens[1].rearrange("(p n) k -> p n k", n=NT))
-        raw_s1 = load("raw_s1", sat_tokens[1].rearrange("(n p) k -> p n k", p=P))
+        raw = {}
+        raw["wq"] = load("raw_wq", Wq.rearrange("(p n) k -> p n k", n=NT))
+        raw["d0"] = load("raw_d0", drone_tokens[0].rearrange("(p n) k -> p n k", n=NT))
+        raw["wk"] = load("raw_wk", Wk.rearrange("(p n) k -> p n k", n=NT))
+        raw["s0"] = load("raw_s0", sat_tokens[0].rearrange("(n p) k -> p n k", p=P))
+        raw["d1"] = load("raw_d1", drone_tokens[1].rearrange("(p n) k -> p n k", n=NT))
+        raw["s1"] = load("raw_s1", sat_tokens[1].rearrange("(n p) k -> p n k", p=P))
 
-        def mx_tiles(name):
-            codes = keep.tile([P, D], U32, name="c_" + name, align_bytes=64)
-            scales = keep.tile([P, D], U8, name="s_" + name, align_bytes=64)
-            return codes, scales
+        ident_f = const.tile([P, P], F32, name="ident_f")
+        make_identity(nc, ident_f[:])
+        ident_b = const.tile([P, P], BF16, name="ident_b")
+        make_identity(nc, ident_b[:])
+        ones_b = const.tile([P, P], BF16, name="ones_b")
+        nc.vector.memset(ones_b[:], 1.0)
+        negh_f = const.tile([P, P], F32, name="negh_f")
+        nc.vector.memset(negh_f[:], -1.0 / B)
+        neg10 = const.tile([P, 1], F32, name="neg10")
+        nc.vector.memset(neg10[:], -10.0)
+        mhalf = const.tile([P, NT], F32, name="mhalf")
+        nc.vector.memset(mhalf[:], -0.5)
+        warm = const.tile([P, 1], F32, name="warm")
+        nc.scalar.activation(out=warm[:], in_=neg10[:], func=ACT.Exp)
 
-        def quantise(grouped, cs):
-            nc.vector.quantize_mx(out=cs[0][:].bitcast(FP8X4), scales=cs[1][:], in_=grouped[:])
-
-        def pack_input(raw, name):
-            cs = mx_tiles(name)
-            words = raw[:].bitcast(F32)
-            grouped = grp.tile([P, NT * P * 4], BF16, tag="grouped", align_bytes=64)
-            gw = grouped[:].bitcast(F32).rearrange("p (h r w u) -> p h r w u", h=2, r=2, w=P, u=2)
-            for h in range(2):
-                xt = ps_tp.tile([P, 2, 2, P], F32, tag="tp")
-                for r in range(2):
-                    for u in range(2):
-                        col = (2 * h + r) * 256 + u * P
-                        nc.tensor.transpose(xt[:, r, u, :], words[:, col:col + P], ident_f[:])
-                evac(gw[:, h], xt[:].rearrange("p r u w -> p r w u"))
-            quantise(grouped, cs)
-            return cs
+        bias = []
 
         def bias_tile(i):
-            ps = ps_mm.tile([P, D], F32, tag="mm")
+            ps = ps_f.tile([P, D], F32, tag="f")
             nc.tensor.matmul(out=ps[:], lhsT=ones_b[:], rhs=brows[i][:], start=True, stop=True)
             bias_sb = const.tile([P, D], F32, name="bias%d" % i)
-            nc.vector.tensor_copy(
-                out=bias_sb[:].rearrange("p (n q) -> p n q", n=NT),
-                in_=ps[:].rearrange("p (q n) -> p n q", n=NT),
+            copy_on(
+                "SV"[i],
+                bias_sb[:].rearrange("p (n q) -> p n q", n=NT),
+                ps[:].rearrange("p (q n) -> p n q", n=NT),
             )
-            return bias_sb
+            bias.append(bias_sb)
 
-        def project(tok, w, bias_sb, g):
-            ss = keep.tile([P, NT], F32, name="ss" + g)
-            ys = []
-            for n in range(NT):
-                z = ps_mm.tile([P, D], F32, tag="mm")
-                nc.tensor.matmul_mx(
-                    out=z[:],
-                    lhsT=tok[0][:, n * P:(n + 1) * P].bitcast(FP8X4),
-                    lhsT_scale=tok[1][:, n * P:(n + 1) * P],
-                    rhs=w[0][:].bitcast(FP8X4),
-                    rhs_scale=w[1][:],
-                    start=True,
-                    stop=True,
-                )
-                y = ypool.tile([P, D], F32, tag="y")
-                nc.vector.tensor_tensor(out=y[:], in0=z[:], in1=bias_sb[:], op=ALU.add)
-                sq = junk.tile([P, D], BF16, tag="sq")
-                nc.scalar.activation(out=sq[:], in_=y[:], func=ACT.Square, accum_out=ss[:, n:n + 1])
-                ys.append(y)
-            ssc = keep.tile([P, NT], F32, name="ssc" + g)
-            nc.vector.tensor_scalar_max(out=ssc[:], in0=ss[:], scalar1=1e-24)
-            nrm = keep.tile([P, NT], F32, name="nrm" + g)
-            nc.scalar.activation(out=nrm[:], in_=ssc[:], func=ACT.Sqrt)
-            rn = keep.tile([P, NT], F32, name="rn" + g)
-            nc.vector.reciprocal(out=rn[:], in_=nrm[:])
-            qbs = []
-            for n in range(NT):
-                qb = keep.tile([P, D], BF16, name="qb%s_%d" % (g, n))
+        codes = {}
+        grouped = {}
+        bank = {}
+
+        def mx_tiles(name):
+            c = keep.tile([P, D], U32, name="c_" + name, align_bytes=64)
+            s = keep.tile([P, D], U8, name="s_" + name, align_bytes=64)
+            codes[name] = (c, s)
+
+        def quantise(name):
+            c, s = codes[name]
+            nc.vector.quantize_mx(out=c[:].bitcast(FP8X4), scales=s[:], in_=grouped[name][:])
+
+        def in_T(x, h):
+            if h == 0:
+                mx_tiles(x)
+                g = grp.tile([P, NT * P * 4], BF16, tag="grouped", align_bytes=64)
+                grouped[x] = g
+            words = raw[x][:].bitcast(F32)
+            xt = ps_f.tile([P, 2, 2, P], F32, tag="f")
+            for r in range(2):
+                for u in range(2):
+                    col = (2 * h + r) * 256 + u * P
+                    nc.tensor.transpose(xt[:, r, u, :], words[:, col:col + P], ident_f[:])
+            bank[(x, h)] = xt
+
+        def in_E(x, h, eng):
+            gw = grouped[x][:].bitcast(F32).rearrange("p (h r w u) -> p h r w u", h=2, r=2, w=P, u=2)
+            copy_on(eng, gw[:, h], bank[(x, h)][:].rearrange("p r u w -> p r w u"))
+
+        ys = {}
+        qbs = {}
+        ss = {}
+        rn = {}
+
+        def pr_M(c, w, n):
+            z = ps_f.tile([P, D], F32, tag="f")
+            nc.tensor.matmul_mx(
+                out=z[:],
+                lhsT=codes[c][0][:, n * P:(n + 1) * P].bitcast(FP8X4),
+                lhsT_scale=codes[c][1][:, n * P:(n + 1) * P],
+                rhs=codes[w][0][:].bitcast(FP8X4),
+                rhs_scale=codes[w][1][:],
+                start=True,
+                stop=True,
+            )
+            bank[(c, "z", n)] = z
+
+        def pr_A(c, bi, n):
+            y = ypool.tile([P, D], F32, tag="y")
+            nc.vector.tensor_tensor(out=y[:], in0=bank[(c, "z", n)][:], in1=bias[bi][:], op=ALU.add)
+            ys[(c, n)] = y
+
+        def pr_S(c, n):
+            if n == 0:
+                ss[c] = keep.tile([P, NT], F32, name="ss" + c)
+            sq = junk.tile([P, D], BF16, tag="sq")
+            nc.scalar.activation(out=sq[:], in_=ys[(c, n)][:], func=ACT.Square, accum_out=ss[c][:, n:n + 1])
+
+        def pr_R(c):
+            rn[c] = keep.tile([P, NT], F32, name="rn" + c)
+            ssc = keep.tile([P, NT], F32, name="ssc" + c)
+            nc.gpsimd.tensor_scalar(out=ssc[:], in0=ss[c][:], scalar1=1e-24, scalar2=0.0, op0=ALU.max, op1=ALU.add)
+            nc.gpsimd.tensor_tensor(out=rn[c][:], in0=ssc[:], in1=mhalf[:], op=ALU.pow)
+
+        def pr_C(c, n, eng):
+            qb = qpool.tile([P, D], BF16, tag="qb")
+            if eng == "G":
                 nc.gpsimd.tensor_scalar(
-                    out=qb[:], in0=ys[n][:], scalar1=rn[:, n:n + 1], scalar2=0.0, op0=ALU.mult, op1=ALU.add
+                    out=qb[:], in0=ys[(c, n)][:], scalar1=rn[c][:, n:n + 1], scalar2=0.0, op0=ALU.mult, op1=ALU.add
                 )
-                qbs.append(qb)
-            return qbs
+            elif eng == "V":
+                nc.vector.tensor_scalar(
+                    out=qb[:], in0=ys[(c, n)][:], scalar1=rn[c][:, n:n + 1], scalar2=0.0, op0=ALU.mult, op1=ALU.add
+                )
+            else:
+                nc.scalar.activation(out=qb[:], in_=ys[(c, n)][:], func=ACT.Copy, scale=rn[c][:, n:n + 1])
+            qbs[(c, n)] = qb
 
-        def pack_features(qbs, name):
-            cs = mx_tiles(name)
-            grouped = grp.tile([P, NT * P * 4], BF16, tag="grouped", align_bytes=64)
-            gv = grouped[:].rearrange("p (h r w t) -> p h r w t", h=2, r=2, w=P, t=4)
-            for h in range(2):
-                qt = ps_qt.tile([P, 2, NT, P], BF16, tag="qt")
-                for r in range(2):
-                    for t in range(NT):
-                        nc.tensor.transpose(qt[:, r, t, :], qbs[2 * h + r][:, t * P:(t + 1) * P], ident_b[:])
-                evac(gv[:, h], qt[:].rearrange("p r t w -> p r w t"))
-            quantise(grouped, cs)
-            return cs
+        def ft_T(c, h):
+            if h == 0:
+                mx_tiles("n" + c)
+                g = grp.tile([P, NT * P * 4], BF16, tag="grouped", align_bytes=64)
+                grouped["n" + c] = g
+            qt = ps_b.tile([P, 2, NT, P], BF16, tag="b")
+            for r in range(2):
+                for t in range(NT):
+                    nc.tensor.transpose(qt[:, r, t, :], qbs[(c, 2 * h + r)][:, t * P:(t + 1) * P], ident_b[:])
+            bank[(c, "qt", h)] = qt
 
-        cwq = pack_input(raw_wq, "wq")
-        cd0 = pack_input(raw_d0, "d0")
-        bias_q = bias_tile(0)
-        q0 = project(cd0, cwq, bias_q, "d0")
-        cwk = pack_input(raw_wk, "wk")
-        cs0 = pack_input(raw_s0, "s0")
-        bias_k = bias_tile(1)
-        k0 = project(cs0, cwk, bias_k, "s0")
-        cq0 = pack_features(q0, "q0")
-        cd1 = pack_input(raw_d1, "d1")
-        q1 = project(cd1, cwq, bias_q, "d1")
-        ck0 = pack_features(k0, "k0")
-        cs1 = pack_input(raw_s1, "s1")
-        k1 = project(cs1, cwk, bias_k, "s1")
-        cq1 = pack_features(q1, "q1")
-        ck1 = pack_features(k1, "k1")
-        cq = [cq0, cq1]
-        ck = [ck0, ck1]
+        def ft_E(c, h, eng):
+            gv = grouped["n" + c][:].rearrange("p (h r w t) -> p h r w t", h=2, r=2, w=P, t=4)
+            copy_on(eng, gv[:, h], bank[(c, "qt", h)][:].rearrange("p r t w -> p r w t"))
 
-        E = [[], []]
-        C = [[], []]
-        KH = [[], []]
-        KL = [[], []]
-        rsum = []
-        for b in range(B):
-            r1 = keep.tile([P, NT], F32, name="r1_%d" % b)
-            rsum.append(r1)
-            for n in range(NT):
-                z = ps_mm.tile([P, D], F32, tag="mm")
+        E = {}
+        GC = {}
+        KH = {}
+        KL = {}
+        KT = {}
+        r1 = {}
+
+        def cs_M(b, n):
+            z = ps_f.tile([P, D], F32, tag="f")
+            cq = codes["nd%d" % b]
+            ck = codes["ns%d" % b]
+            nc.tensor.matmul_mx(
+                out=z[:],
+                lhsT=cq[0][:, n * P:(n + 1) * P].bitcast(FP8X4),
+                lhsT_scale=cq[1][:, n * P:(n + 1) * P],
+                rhs=ck[0][:].bitcast(FP8X4),
+                rhs_scale=ck[1][:],
+                start=True,
+                stop=True,
+            )
+            bank[(b, "c", n)] = z
+
+        def cs_X(b, n):
+            if n == 0:
+                r1[b] = keep.tile([P, NT], F32, name="r1_%d" % b)
+            e = keep.tile([P, D], F32, name="e%d_%d" % (b, n))
+            nc.scalar.activation(
+                out=e[:], in_=bank[(b, "c", n)][:], func=ACT.Exp, scale=10.0, bias=neg10[:],
+                accum_out=r1[b][:, n:n + 1],
+            )
+            E[(b, n)] = e
+
+        def cs_G(b, n):
+            g = keep.tile([P, D], F32, name="g%d_%d" % (b, n))
+            nc.vector.scalar_tensor_tensor(
+                out=g[:], in0=bank[(b, "c", n)][:], scalar=-1.0, in1=E[(b, n)][:], op0=ALU.add, op1=ALU.mult
+            )
+            GC[(b, n)] = g
+
+        def cs_H(b, n, eng):
+            kh = keep.tile([P, D], BF16, name="kh%d_%d" % (b, n))
+            if eng == "G":
+                nc.gpsimd.tensor_scalar(out=kh[:], in0=E[(b, n)][:], scalar1=1.0, scalar2=0.0, op0=ALU.mult, op1=ALU.add)
+            else:
+                copy_on(eng, kh[:], E[(b, n)][:])
+            KH[(b, n)] = kh
+
+        def cs_L(b, n):
+            kl = keep.tile([P, D], BF16, name="kl%d_%d" % (b, n))
+            if L_ENG[b][n] == "V":
+                nc.vector.tensor_tensor(out=kl[:], in0=E[(b, n)][:], in1=KH[(b, n)][:], op=ALU.subtract)
+            else:
+                nc.gpsimd.tensor_tensor(out=kl[:], in0=E[(b, n)][:], in1=KH[(b, n)][:], op=ALU.subtract)
+            KL[(b, n)] = kl
+
+        def et_T(b, n):
+            if n == 0:
+                KT[b] = keep.tile([P, NT, 2, NT, P], BF16, name="kt%d" % b)
+            kt_ps = ps_b.tile([P, 2, NT, P], BF16, tag="b")
+            for s, src in enumerate((KH, KL)):
+                for m in range(NT):
+                    nc.tensor.transpose(kt_ps[:, s, m, :], src[(b, n)][:, m * P:(m + 1) * P], ident_b[:])
+            bank[(b, "kt", n)] = kt_ps
+
+        def et_E(b, n, eng):
+            copy_on(eng, KT[b][:, :, :, n, :], bank[(b, "kt", n)][:].rearrange("p s m i -> p m s i"))
+
+        def dummy(k, name):
+            for i_ in range(k):
+                jz = ps_f.tile([P, D], F32, tag="f")
+                cw = codes[name]
                 nc.tensor.matmul_mx(
-                    out=z[:],
-                    lhsT=cq[b][0][:, n * P:(n + 1) * P].bitcast(FP8X4),
-                    lhsT_scale=cq[b][1][:, n * P:(n + 1) * P],
-                    rhs=ck[b][0][:].bitcast(FP8X4),
-                    rhs_scale=ck[b][1][:],
-                    start=True,
-                    stop=True,
+                    out=jz[:], lhsT=cw[0][:, 0:P].bitcast(FP8X4), lhsT_scale=cw[1][:, 0:P],
+                    rhs=cw[0][:].bitcast(FP8X4), rhs_scale=cw[1][:], start=True, stop=True,
                 )
-                e = keep.tile([P, D], F32, name="e%d_%d" % (b, n))
-                nc.scalar.activation(
-                    out=e[:], in_=z[:], func=ACT.Exp, scale=10.0, bias=neg10[:], accum_out=r1[:, n:n + 1]
-                )
-                c = keep.tile([P, D], F32, name="c%d_%d" % (b, n))
-                nc.vector.tensor_scalar(out=c[:], in0=z[:], scalar1=-1.0, scalar2=1.0, op0=ALU.mult, op1=ALU.add)
-                kh = keep.tile([P, D], BF16, name="kh%d_%d" % (b, n))
-                nc.gpsimd.tensor_scalar(out=kh[:], in0=e[:], scalar1=1.0, scalar2=0.0, op0=ALU.mult, op1=ALU.add)
-                kl = keep.tile([P, D], BF16, name="kl%d_%d" % (b, n))
-                nc.gpsimd.tensor_tensor(out=kl[:], in0=e[:], in1=kh[:], op=ALU.subtract)
-                E[b].append(e)
-                C[b].append(c)
-                KH[b].append(kh)
-                KL[b].append(kl)
-
-        def transpose_kernel(b):
-            kts = []
-            for m in range(NT):
-                kt_ps = ps_qt.tile([P, 2, NT, P], BF16, tag="qt")
-                for s, src in enumerate((KH[b], KL[b])):
-                    for n in range(NT):
-                        nc.tensor.transpose(kt_ps[:, s, n, :], src[n][:, m * P:(m + 1) * P], ident_b[:])
-                kt = keep.tile([P, 2, NT, P], BF16, name="kt%d_%d" % (b, m))
-                evac(kt[:], kt_ps[:])
-                kts.append(kt)
-            return kts
 
         def invert(s, b):
             v = vec.tile([P, NT], F32, tag="v%d" % b)
             nc.vector.reciprocal(out=v[:], in_=s)
             hl = vec.tile([P, NT, 2], BF16, tag="hl%d" % b)
-            nc.vector.tensor_copy(out=hl[:, :, 0], in_=v[:])
+            with nc.allow_low_precision(reason="high half of a two-term bfloat16 split; the low half takes up the rest"):
+                nc.vector.reciprocal(out=hl[:, :, 0], in_=s)
             nc.vector.tensor_tensor(out=hl[:, :, 1], in0=v[:], in1=hl[:, :, 0], op=ALU.subtract)
             return v, hl
 
         def matvec(b, stationary, hl):
-            acc = ps_tp.tile([P, NT, 2], F32, tag="tp")
+            acc = ps_f.tile([P, NT, 2], F32, tag="f")
             for m in range(NT):
                 for c in range(NT):
                     for s in range(2):
@@ -238,58 +290,116 @@ def tile_sinkhornot_kernel(tc, drone_tokens, sat_tokens, Wq, bq, Wk, bk, out_0, 
                             start=(c == 0 and s == 0),
                             stop=(c == NT - 1 and s == 1),
                         )
+            return acc
+
+        def chain(b, acc):
             tot = vec.tile([P, NT], F32, tag="tot%d" % b)
             nc.vector.tensor_reduce(out=tot[:], in_=acc[:], axis=AX.X, op=ALU.add)
             return invert(tot[:], b)
 
-        KT = [None, None]
+        def col_stat(b):
+            return lambda s, c, m: (KH, KL)[s][(b, c)][:, m * P:(m + 1) * P]
+
+        def row_stat(b):
+            return lambda s, c, m: KT[b][:, c, s, m, :]
+
+        plan_ = []
+
+        def at(t, fn, *args):
+            plan_.append((t, len(plan_), fn, args))
+
+        ARR = {"wq": 2.9, "d0": 3.9, "wk": 4.9, "s0": 5.9, "d1": 6.9, "s1": 7.9}
+        for x in ARR:
+            for h in range(2):
+                at(ARR[x] + 0.3 * h, in_T, x, h)
+                at(ARR[x] + 0.7 + 0.1 * h, in_E, x, h, IE_ENG[x][h])
+            at(ARR[x] + QI_OFF, quantise, x)
+            if x not in ("wq", "d0"):
+                at(ARR[x] + 0.35, dummy, DUM["in"], "wq")
+        at(2.0, bias_tile, 0)
+        at(2.1, bias_tile, 1)
+        chains = ("d0", "s0", "d1", "s1")
+        wof = {"d0": "wq", "s0": "wk", "d1": "wq", "s1": "wk"}
+        bof = {"d0": 0, "s0": 1, "d1": 0, "s1": 1}
+        for i, c in enumerate(chains):
+            t0 = CH[i]
+            for n in range(NT):
+                at(t0 + 0.25 * n, pr_M, c, wof[c], n)
+                at(t0 + OFF["A"] + 0.45 * n, pr_A, c, bof[c], n)
+                at(t0 + OFF["S"] + 0.45 * n, pr_S, c, n)
+            at(t0 + OFF["R"], pr_R, c)
+            for n in range(NT):
+                at(t0 + OFF["C"] + OFF["dC"] * n, pr_C, c, n, SCALE_ENG[i][n])
+            for h in range(2):
+                at(t0 + OFF["FT"] + OFF["dF"] * h, ft_T, c, h)
+                at(t0 + OFF["FE"] + OFF["dF"] * h, ft_E, c, h, FE_ENG[i][h])
+                at(t0 + OFF["FT"] + OFF["dF"] * h + 0.01, dummy, DUM["ft"], "wq")
+            at(t0 + OFF["QF"], quantise, "n" + c)
+        for b in range(B):
+            t2 = CS[b]
+            for n in range(NT):
+                at(t2 + 0.25 * n, cs_M, b, n)
+                at(t2 + OFF["X"] + 0.5 * n, cs_X, b, n)
+                at(t2 + OFF["H"] + 0.5 * n, cs_H, b, n, H_ENG[b][n])
+                at(t2 + OFF["G"] + 0.5 * n, cs_G, b, n)
+                at(t2 + OFF["L"] + 0.5 * n, cs_L, b, n)
+                at(t2 + OFF["ET"] + 0.5 * n, et_T, b, n)
+                at(t2 + OFF["EE"] + 0.5 * n, et_E, b, n, "S")
+                at(t2 + OFF["ET"] + 0.5 * n + 0.01, dummy, DUM["et"], "wq")
+        for t, i, fn, args in sorted(plan_):
+            fn(*args)
+
         av = [None, None]
         bv = [None, None]
         for b in range(B):
-            av[b] = invert(rsum[b][:], b)
-
-        def col_stat(b):
-            return lambda s, c, m: (KH[b], KL[b])[s][c][:, m * P:(m + 1) * P]
-
-        def row_stat(b):
-            return lambda s, c, m: KT[b][c][:, s, m, :]
+            av[b] = invert(r1[b][:], b)
 
         for it in range(ITERS):
             if it > 0:
                 for b in range(B):
-                    av[b] = matvec(b, row_stat(b), bv[b][1])
+                    acc = matvec(b, row_stat(b), bv[b][1])
+                    dummy(DUM["sk"][b], "wq")
+                    av[b] = chain(b, acc)
             for b in range(B):
-                bv[b] = matvec(b, col_stat(b), av[b][1])
-                if it == 0:
-                    KT[b] = transpose_kernel(b)
+                acc = matvec(b, col_stat(b), av[b][1])
+                dummy(DUM["sk"][b], "wq")
+                bv[b] = chain(b, acc)
 
-        otp = keep.tile([P, B * NT], F32, name="otp")
+        otp = keep.tile([P, B], F32, name="otp")
         for b in range(B):
-            bb = ps_mm.tile([P, D], F32, tag="mm")
+            bb = ps_f.tile([P, D], F32, tag="f")
             for m in range(NT):
                 nc.tensor.transpose(
                     bb[:, m * P:(m + 1) * P], bv[b][0][:, m:m + 1].to_broadcast([P, P]), ident_f[:]
                 )
             dst = out_0[b].rearrange("(p n) j -> p n j", n=NT)
             for n in range(NT):
-                ka = keep.tile([P, D], F32, name="ka%d_%d" % (b, n))
-                nc.scalar.activation(out=ka[:], in_=E[b][n][:], func=ACT.Copy, scale=av[b][0][:, n:n + 1])
                 plan = outp.tile([P, D], F32, tag="plan")
-                nc.vector.tensor_tensor(out=plan[:], in0=ka[:], in1=bb[:], op=ALU.mult)
-                nc.sync.dma_start(out=dst[:, n, :], in_=plan[:])
-                pc = junk.tile([P, D], F32, tag="pc")
                 nc.vector.scalar_tensor_tensor(
-                    out=pc[:], in0=plan[:], scalar=1.0, in1=C[b][n][:], op0=ALU.mult, op1=ALU.mult,
-                    accum_out=otp[:, b * NT + n:b * NT + n + 1],
+                    out=plan[:], in0=E[(b, n)][:], scalar=av[b][0][:, n:n + 1], in1=bb[:], op0=ALU.mult, op1=ALU.mult
                 )
-
-        tot2 = keep.tile([P, 2], F32, name="tot2")
-        nc.vector.memset(tot2[:], 0.0)
-        nc.vector.tensor_reduce(out=tot2[:, 0:1], in_=otp[:], axis=AX.X, op=ALU.add)
-        fin = ps_tp.tile([P, 2], F32, tag="tp")
-        nc.tensor.matmul(out=fin[:], lhsT=ones_f[:], rhs=tot2[:], start=True, stop=True)
+                nc.sync.dma_start(out=dst[:, n, :], in_=plan[:])
+        for b in range(B):
+            wacc = ps_f.tile([P, NT], F32, tag="f")
+            for m in range(NT):
+                for c in range(NT):
+                    nc.tensor.matmul(
+                        out=wacc[:, m:m + 1],
+                        lhsT=GC[(b, c)][:, m * P:(m + 1) * P],
+                        rhs=av[b][0][:, c:c + 1],
+                        start=(c == 0),
+                        stop=(c == NT - 1),
+                    )
+            wj = vec.tile([P, NT], F32, tag="wj")
+            nc.vector.scalar_tensor_tensor(
+                out=wj[:], in0=wacc[:], scalar=1.0, in1=bv[b][0][:], op0=ALU.mult, op1=ALU.mult,
+                accum_out=otp[:, b:b + 1],
+            )
+        fin = ps_f.tile([P, 1], F32, tag="f")
+        for b in range(B):
+            nc.tensor.matmul(out=fin[:], lhsT=negh_f[:], rhs=otp[:, b:b + 1], start=(b == 0), stop=(b == B - 1))
         res = keep.tile([P, 1], F32, name="res")
-        nc.scalar.mul(out=res[:], in_=fin[:, 0:1], mul=1.0 / B)
+        nc.vector.tensor_copy(out=res[:], in_=fin[:])
         o1 = out_1
         while len(o1.shape) < 2:
             o1 = o1.unsqueeze(0)

@@ -18,14 +18,18 @@ NT = 4
 B = 2
 ITERS = 5
 QI_OFF = 1.3
-IE_ENG = {"wq":"SV","d0":"SV","wk":"SS","s0":"SS","d1":"VS","s1":"SS"}
-L_ENG = ("VGVG","VGVV")
-CH = (5.5,7.5,10,12.3)
-CS = (19.3,21.5)
-SCALE_ENG = ("GVSG","GVGG","SGGS","GVVG")
-FE_ENG = ("SV","SS","SS","SV")
-H_ENG = ("VSSS","SVSS")
-OFF = {"A":0.4,"S":1.1,"R":3.2,"C":3.9,"dC":0.6,"FT":5,"dF":1.2,"FE":6.1,"QF":8,"X":0.6,"H":1.3,"G":1.7,"L":1.8,"ET":2.6,"EE":3.9}
+BIAS_T = 5.3
+NF = 6
+FILL = (1,1,1)
+LAG = 1
+IE_ENG = {"wq":"SV","d0":"SV","wk":"SS","s0":"SS","d1":"SS","s1":"VS"}
+L_ENG = ("VVVV","VVVG")
+CH = (5.7,7.3,9.8,11.4)
+CS = (19.2,21.2)
+SCALE_ENG = ("VVVS","VGGV","GSVS","GSGV")
+FE_ENG = ("SV","SV","VS","SV")
+H_ENG = ("VVVS","VVVS")
+OFF = {"A":0.2,"S":1.1,"R":2.7,"C":3.7,"dC":0.6,"FT":5.9,"dF":1,"FE":6.1,"QF":7.8,"X":0.8,"H":1.3,"G":1.1,"L":1.8,"ET":2.4,"EE":2.9}
 DUM = {"in": 0, "ft": 0, "et": 0, "sk": (0, 0)}
 FLOPS = 2 * 2 * (B * 512) * D * D + 2 * B * 512 * 512 * D
 
@@ -36,14 +40,14 @@ def tile_sinkhornot_kernel(tc, drone_tokens, sat_tokens, Wq, bq, Wk, bk, out_0, 
         ctx.enter_context(tc.manual_schedule())
         const = ctx.enter_context(tc.tile_pool(name="const", bufs=1))
         keep = ctx.enter_context(tc.tile_pool(name="keep", bufs=1))
-        grp = ctx.enter_context(tc.tile_pool(name="grp", bufs=3))
-        ypool = ctx.enter_context(tc.tile_pool(name="ypool", bufs=12))
-        qpool = ctx.enter_context(tc.tile_pool(name="qpool", bufs=12))
+        grp = ctx.enter_context(tc.tile_pool(name="grp", bufs=4))
+        ypool = ctx.enter_context(tc.tile_pool(name="ypool", bufs=16))
+        qpool = ctx.enter_context(tc.tile_pool(name="qpool", bufs=16))
         junk = ctx.enter_context(tc.tile_pool(name="junk", bufs=2))
         vec = ctx.enter_context(tc.tile_pool(name="vec", bufs=3))
-        outp = ctx.enter_context(tc.tile_pool(name="outp", bufs=4))
-        ps_f = ctx.enter_context(tc.psum_pool(name="ps_f", bufs=6))
-        ps_b = ctx.enter_context(tc.psum_pool(name="ps_b", bufs=2))
+        outp = ctx.enter_context(tc.tile_pool(name="outp", bufs=8))
+        ps_f = ctx.enter_context(tc.psum_pool(name="ps_f", bufs=NF))
+        ps_b = ctx.enter_context(tc.psum_pool(name="ps_b", bufs=8 - NF))
 
         def copy_on(eng, out, in_):
             if eng == "V":
@@ -52,10 +56,9 @@ def tile_sinkhornot_kernel(tc, drone_tokens, sat_tokens, Wq, bq, Wk, bk, out_0, 
                 nc.scalar.copy(out=out, in_=in_)
 
         brows = []
-        for i, bvec in enumerate((bq, bk)):
+        for i in range(2):
             brow = const.tile([P, D], BF16, name="brow%d" % i)
             nc.vector.memset(brow[:], 0.0)
-            nc.scalar.dma_start(out=brow[0:1, :], in_=bvec.rearrange("(o f) -> o f", o=1))
             brows.append(brow)
 
         def load(name, view):
@@ -66,6 +69,8 @@ def tile_sinkhornot_kernel(tc, drone_tokens, sat_tokens, Wq, bq, Wk, bk, out_0, 
         raw = {}
         raw["wq"] = load("raw_wq", Wq.rearrange("(p n) k -> p n k", n=NT))
         raw["d0"] = load("raw_d0", drone_tokens[0].rearrange("(p n) k -> p n k", n=NT))
+        for i, bvec in enumerate((bq, bk)):
+            nc.sync.dma_start(out=brows[i][0:1, :], in_=bvec.rearrange("(o f) -> o f", o=1))
         raw["wk"] = load("raw_wk", Wk.rearrange("(p n) k -> p n k", n=NT))
         raw["s0"] = load("raw_s0", sat_tokens[0].rearrange("(n p) k -> p n k", p=P))
         raw["d1"] = load("raw_d1", drone_tokens[1].rearrange("(p n) k -> p n k", n=NT))
@@ -225,12 +230,14 @@ def tile_sinkhornot_kernel(tc, drone_tokens, sat_tokens, Wq, bq, Wk, bk, out_0, 
             )
             E[(b, n)] = e
 
-        def cs_G(b, n):
-            g = keep.tile([P, D], F32, name="g%d_%d" % (b, n))
+        def cs_G(b, n, half):
+            if half == 0:
+                GC[(b, n)] = keep.tile([P, D], F32, name="g%d_%d" % (b, n))
+            cols = slice(half * (D // 2), (half + 1) * (D // 2))
             nc.vector.scalar_tensor_tensor(
-                out=g[:], in0=bank[(b, "c", n)][:], scalar=-1.0, in1=E[(b, n)][:], op0=ALU.add, op1=ALU.mult
+                out=GC[(b, n)][:, cols], in0=bank[(b, "c", n)][:, cols], scalar=-1.0, in1=E[(b, n)][:, cols],
+                op0=ALU.add, op1=ALU.mult,
             )
-            GC[(b, n)] = g
 
         def cs_H(b, n, eng):
             kh = keep.tile([P, D], BF16, name="kh%d_%d" % (b, n))
@@ -240,13 +247,29 @@ def tile_sinkhornot_kernel(tc, drone_tokens, sat_tokens, Wq, bq, Wk, bk, out_0, 
                 copy_on(eng, kh[:], E[(b, n)][:])
             KH[(b, n)] = kh
 
-        def cs_L(b, n):
+        def cs_L(b, n, eng):
             kl = keep.tile([P, D], BF16, name="kl%d_%d" % (b, n))
-            if L_ENG[b][n] == "V":
+            if eng == "V":
                 nc.vector.tensor_tensor(out=kl[:], in0=E[(b, n)][:], in1=KH[(b, n)][:], op=ALU.subtract)
             else:
                 nc.gpsimd.tensor_tensor(out=kl[:], in0=E[(b, n)][:], in1=KH[(b, n)][:], op=ALU.subtract)
             KL[(b, n)] = kl
+
+        GH = {}
+        GL = {}
+
+        def g_H(b, n):
+            gh = keep.tile([P, D], BF16, name="gh%d_%d" % (b, n))
+            nc.scalar.copy(out=gh[:], in_=GC[(b, n)][:])
+            GH[(b, n)] = gh
+
+        def g_L(b, n, half):
+            if half == 0:
+                GL[(b, n)] = keep.tile([P, D], BF16, name="gl%d_%d" % (b, n))
+            cols = slice(half * (D // 2), (half + 1) * (D // 2))
+            nc.vector.tensor_tensor(
+                out=GL[(b, n)][:, cols], in0=GC[(b, n)][:, cols], in1=GH[(b, n)][:, cols], op=ALU.subtract
+            )
 
         def et_T(b, n):
             if n == 0:
@@ -269,13 +292,30 @@ def tile_sinkhornot_kernel(tc, drone_tokens, sat_tokens, Wq, bq, Wk, bk, out_0, 
                     rhs=cw[0][:].bitcast(FP8X4), rhs_scale=cw[1][:], start=True, stop=True,
                 )
 
-        def invert(s, b):
+        fillers = []
+
+        taken = [0]
+
+        def fill(k=1):
+            for i_ in range(k):
+                while taken[0] < len(fillers):
+                    on_vector, fn, args = fillers[taken[0]]
+                    taken[0] += 1
+                    fn(*args)
+                    if on_vector:
+                        break
+
+        def invert(s, b, split=True):
             v = vec.tile([P, NT], F32, tag="v%d" % b)
             nc.vector.reciprocal(out=v[:], in_=s)
+            if not split:
+                return v, None
             hl = vec.tile([P, NT, 2], BF16, tag="hl%d" % b)
             with nc.allow_low_precision(reason="high half of a two-term bfloat16 split; the low half takes up the rest"):
                 nc.vector.reciprocal(out=hl[:, :, 0], in_=s)
+            fill(FILL[1])
             nc.vector.tensor_tensor(out=hl[:, :, 1], in0=v[:], in1=hl[:, :, 0], op=ALU.subtract)
+            fill(FILL[2])
             return v, hl
 
         def matvec(b, stationary, hl):
@@ -292,10 +332,11 @@ def tile_sinkhornot_kernel(tc, drone_tokens, sat_tokens, Wq, bq, Wk, bk, out_0, 
                         )
             return acc
 
-        def chain(b, acc):
+        def chain(b, acc, split=True):
             tot = vec.tile([P, NT], F32, tag="tot%d" % b)
             nc.vector.tensor_reduce(out=tot[:], in_=acc[:], axis=AX.X, op=ALU.add)
-            return invert(tot[:], b)
+            fill(FILL[0])
+            return invert(tot[:], b, split)
 
         def col_stat(b):
             return lambda s, c, m: (KH, KL)[s][(b, c)][:, m * P:(m + 1) * P]
@@ -316,8 +357,8 @@ def tile_sinkhornot_kernel(tc, drone_tokens, sat_tokens, Wq, bq, Wk, bk, out_0, 
             at(ARR[x] + QI_OFF, quantise, x)
             if x not in ("wq", "d0"):
                 at(ARR[x] + 0.35, dummy, DUM["in"], "wq")
-        at(2.0, bias_tile, 0)
-        at(2.1, bias_tile, 1)
+        at(BIAS_T, bias_tile, 0)
+        at(BIAS_T + 0.1, bias_tile, 1)
         chains = ("d0", "s0", "d1", "s1")
         wof = {"d0": "wq", "s0": "wk", "d1": "wq", "s1": "wk"}
         bof = {"d0": 0, "s0": 1, "d1": 0, "s1": 1}
@@ -341,8 +382,7 @@ def tile_sinkhornot_kernel(tc, drone_tokens, sat_tokens, Wq, bq, Wk, bk, out_0, 
                 at(t2 + 0.25 * n, cs_M, b, n)
                 at(t2 + OFF["X"] + 0.5 * n, cs_X, b, n)
                 at(t2 + OFF["H"] + 0.5 * n, cs_H, b, n, H_ENG[b][n])
-                at(t2 + OFF["G"] + 0.5 * n, cs_G, b, n)
-                at(t2 + OFF["L"] + 0.5 * n, cs_L, b, n)
+                at(t2 + OFF["L"] + 0.5 * n, cs_L, b, n, L_ENG[b][n])
                 at(t2 + OFF["ET"] + 0.5 * n, et_T, b, n)
                 at(t2 + OFF["EE"] + 0.5 * n, et_E, b, n, "S")
                 at(t2 + OFF["ET"] + 0.5 * n + 0.01, dummy, DUM["et"], "wq")
@@ -351,6 +391,19 @@ def tile_sinkhornot_kernel(tc, drone_tokens, sat_tokens, Wq, bq, Wk, bk, out_0, 
 
         av = [None, None]
         bv = [None, None]
+        tiles = [(b, n) for b in range(B) for n in range(NT)]
+        for i in range(len(tiles) + LAG):
+            if i < len(tiles):
+                b, n = tiles[i]
+                fillers.append((False, cs_M, (b, n)))
+                fillers.append((True, cs_G, (b, n, 0)))
+                fillers.append((True, cs_G, (b, n, 1)))
+                fillers.append((False, g_H, (b, n)))
+            if i >= LAG:
+                b, n = tiles[i - LAG]
+                fillers.append((True, g_L, (b, n, 0)))
+                fillers.append((True, g_L, (b, n, 1)))
+
         for b in range(B):
             av[b] = invert(r1[b][:], b)
 
@@ -363,44 +416,50 @@ def tile_sinkhornot_kernel(tc, drone_tokens, sat_tokens, Wq, bq, Wk, bk, out_0, 
             for b in range(B):
                 acc = matvec(b, col_stat(b), av[b][1])
                 dummy(DUM["sk"][b], "wq")
-                bv[b] = chain(b, acc)
+                bv[b] = chain(b, acc, it < ITERS - 1)
+        fill(len(fillers))
 
         otp = keep.tile([P, B], F32, name="otp")
+        bbs = []
+        waccs = []
         for b in range(B):
             bb = ps_f.tile([P, D], F32, tag="f")
             for m in range(NT):
                 nc.tensor.transpose(
                     bb[:, m * P:(m + 1) * P], bv[b][0][:, m:m + 1].to_broadcast([P, P]), ident_f[:]
                 )
-            dst = out_0[b].rearrange("(p n) j -> p n j", n=NT)
-            for n in range(NT):
-                plan = outp.tile([P, D], F32, tag="plan")
-                nc.vector.scalar_tensor_tensor(
-                    out=plan[:], in0=E[(b, n)][:], scalar=av[b][0][:, n:n + 1], in1=bb[:], op0=ALU.mult, op1=ALU.mult
-                )
-                nc.sync.dma_start(out=dst[:, n, :], in_=plan[:])
+            bbs.append(bb)
         for b in range(B):
-            wacc = ps_f.tile([P, NT], F32, tag="f")
-            for m in range(NT):
-                for c in range(NT):
-                    nc.tensor.matmul(
-                        out=wacc[:, m:m + 1],
-                        lhsT=GC[(b, c)][:, m * P:(m + 1) * P],
-                        rhs=av[b][0][:, c:c + 1],
-                        start=(c == 0),
-                        stop=(c == NT - 1),
-                    )
-            wj = vec.tile([P, NT], F32, tag="wj")
+            waccs.append(matvec(b, lambda s, c, m, b=b: (GH, GL)[s][(b, c)][:, m * P:(m + 1) * P], av[b][1]))
+
+        def plan_tile(b, n):
+            plan = outp.tile([P, D], F32, tag="plan")
             nc.vector.scalar_tensor_tensor(
-                out=wj[:], in0=wacc[:], scalar=1.0, in1=bv[b][0][:], op0=ALU.mult, op1=ALU.mult,
-                accum_out=otp[:, b:b + 1],
+                out=plan[:], in0=E[(b, n)][:], scalar=av[b][0][:, n:n + 1], in1=bbs[b][:], op0=ALU.mult, op1=ALU.mult
             )
+            nc.sync.dma_start(out=out_0[b].rearrange("(p n) j -> p n j", n=NT)[:, n, :], in_=plan[:])
+
+        def ot_part(b):
+            wj = vec.tile([P, NT, 2], F32, tag="wj")
+            nc.vector.scalar_tensor_tensor(
+                out=wj[:], in0=waccs[b][:], scalar=1.0, in1=bv[b][0][:].unsqueeze(2).to_broadcast([P, NT, 2]),
+                op0=ALU.mult, op1=ALU.mult, accum_out=otp[:, b:b + 1],
+            )
+
+        for n in range(NT):
+            plan_tile(0, n)
+        ot_part(0)
+        plan_tile(1, 0)
+        plan_tile(1, 1)
+        ot_part(1)
         fin = ps_f.tile([P, 1], F32, tag="f")
         for b in range(B):
             nc.tensor.matmul(out=fin[:], lhsT=negh_f[:], rhs=otp[:, b:b + 1], start=(b == 0), stop=(b == B - 1))
+        plan_tile(1, 2)
         res = keep.tile([P, 1], F32, name="res")
         nc.vector.tensor_copy(out=res[:], in_=fin[:])
         o1 = out_1
         while len(o1.shape) < 2:
             o1 = o1.unsqueeze(0)
         nc.sync.dma_start(out=o1, in_=res[0:1, 0:1])
+        plan_tile(1, 3)

@@ -30,7 +30,7 @@ SCALE_ENG = ("VVVS","VGGV","GSVS","GSGV")
 FE_ENG = ("SV","SV","VS","SV")
 H_ENG = ("VVVS","VVVS")
 OFF = {"A":0.2,"S":1.1,"R":2.7,"C":3.7,"dC":0.6,"FT":5.9,"dF":1,"FE":6.1,"QF":7.8,"X":0.8,"H":1.3,"G":1.1,"L":1.8,"ET":2.4,"EE":2.9}
-DUM = {"in": 0, "ft": 0, "et": 0, "sk": (0, 0)}
+DUM = {"in": 0, "ft": 0, "et": 0, "sk": (2, 2)}
 FLOPS = 2 * 2 * (B * 512) * D * D + 2 * B * 512 * 512 * D
 
 

@@ -20,6 +20,8 @@ ITERS = 5
 QI_OFF = 1.3
 BIAS_T = 5.3
 NF = 6
+BIAS_ENG = "SV"
+EE_ENG = ("SSSS", "SSSS")
 FILL = (1,1,1)
 LAG = 1
 IE_ENG = {"wq":"SV","d0":"SV","wk":"SS","s0":"SS","d1":"SS","s1":"VS"}
@@ -29,8 +31,8 @@ CS = (19.2,21.2)
 SCALE_ENG = ("VVVS","VGGV","GSVS","GSGV")
 FE_ENG = ("SV","SV","VS","SV")
 H_ENG = ("VVVS","VVVS")
-OFF = {"A":0.2,"S":1.1,"R":2.7,"C":3.7,"dC":0.6,"FT":5.9,"dF":1,"FE":6.1,"QF":7.8,"X":0.8,"H":1.3,"G":1.1,"L":1.8,"ET":2.4,"EE":2.9}
-DUM = {"in": 0, "ft": 0, "et": 0, "sk": (2, 2)}
+OFF = {"A":0.2,"S":1.1,"R":2.7,"C":3.7,"dC":0.6,"FT":5.9,"dF":1,"FE":6.1,"QF":7.8,"X":0.8,"H":1.3,"G":1.1,"L":1.8,"ET":2.4,"EE":2.9,"IV":2.9}
+DUM = {"in": 0, "ft": 0, "et": 0, "sk": (2, 1)}
 FLOPS = 2 * 2 * (B * 512) * D * D + 2 * B * 512 * 512 * D
 
 
@@ -98,7 +100,7 @@ def tile_sinkhornot_kernel(tc, drone_tokens, sat_tokens, Wq, bq, Wk, bk, out_0, 
             nc.tensor.matmul(out=ps[:], lhsT=ones_b[:], rhs=brows[i][:], start=True, stop=True)
             bias_sb = const.tile([P, D], F32, name="bias%d" % i)
             copy_on(
-                "SV"[i],
+                BIAS_ENG[i],
                 bias_sb[:].rearrange("p (n q) -> p n q", n=NT),
                 ps[:].rearrange("p (q n) -> p n q", n=NT),
             )
@@ -305,7 +307,7 @@ def tile_sinkhornot_kernel(tc, drone_tokens, sat_tokens, Wq, bq, Wk, bk, out_0, 
                     if on_vector:
                         break
 
-        def invert(s, b, split=True):
+        def invert(s, b, split=True, filled=True):
             v = vec.tile([P, NT], F32, tag="v%d" % b)
             nc.vector.reciprocal(out=v[:], in_=s)
             if not split:
@@ -313,9 +315,11 @@ def tile_sinkhornot_kernel(tc, drone_tokens, sat_tokens, Wq, bq, Wk, bk, out_0, 
             hl = vec.tile([P, NT, 2], BF16, tag="hl%d" % b)
             with nc.allow_low_precision(reason="high half of a two-term bfloat16 split; the low half takes up the rest"):
                 nc.vector.reciprocal(out=hl[:, :, 0], in_=s)
-            fill(FILL[1])
+            if filled:
+                fill(FILL[1])
             nc.vector.tensor_tensor(out=hl[:, :, 1], in0=v[:], in1=hl[:, :, 0], op=ALU.subtract)
-            fill(FILL[2])
+            if filled:
+                fill(FILL[2])
             return v, hl
 
         def matvec(b, stationary, hl):
@@ -384,13 +388,19 @@ def tile_sinkhornot_kernel(tc, drone_tokens, sat_tokens, Wq, bq, Wk, bk, out_0, 
                 at(t2 + OFF["H"] + 0.5 * n, cs_H, b, n, H_ENG[b][n])
                 at(t2 + OFF["L"] + 0.5 * n, cs_L, b, n, L_ENG[b][n])
                 at(t2 + OFF["ET"] + 0.5 * n, et_T, b, n)
-                at(t2 + OFF["EE"] + 0.5 * n, et_E, b, n, "S")
+                at(t2 + OFF["EE"] + 0.5 * n, et_E, b, n, EE_ENG[b][n])
                 at(t2 + OFF["ET"] + 0.5 * n + 0.01, dummy, DUM["et"], "wq")
+        av = [None, None]
+        bv = [None, None]
+
+        def first_a(b):
+            av[b] = invert(r1[b][:], b, True, False)
+
+        for b in range(B):
+            at(CS[b] + OFF["IV"], first_a, b)
         for t, i, fn, args in sorted(plan_):
             fn(*args)
 
-        av = [None, None]
-        bv = [None, None]
         tiles = [(b, n) for b in range(B) for n in range(NT)]
         for i in range(len(tiles) + LAG):
             if i < len(tiles):
@@ -403,9 +413,6 @@ def tile_sinkhornot_kernel(tc, drone_tokens, sat_tokens, Wq, bq, Wk, bk, out_0, 
                 b, n = tiles[i - LAG]
                 fillers.append((True, g_L, (b, n, 0)))
                 fillers.append((True, g_L, (b, n, 1)))
-
-        for b in range(B):
-            av[b] = invert(r1[b][:], b)
 
         for it in range(ITERS):
             if it > 0:

@@ -14,26 +14,32 @@ AX = mybir.AxisListType
 
 P = 128
 D = 512
-NT = 4
+NT = D // P
 B = 2
 ITERS = 5
-QI_OFF = 1.3
-BIAS_T = 5.3
-NF = 6
-BIAS_ENG = "SV"
-EE_ENG = ("SSSS", "SSSS")
-FILL = (1,1,1)
-LAG = 1
-IE_ENG = {"wq":"SV","d0":"SV","wk":"SS","s0":"SS","d1":"SS","s1":"VS"}
-L_ENG = ("VVVV","VVVG")
-CH = (5.7,7.3,9.8,11.4)
-CS = (19.2,21.2)
-SCALE_ENG = ("VVVS","VGGV","GSVS","GSGV")
-FE_ENG = ("SV","SV","VS","SV")
-H_ENG = ("VVVS","VVVS")
-OFF = {"A":0.2,"S":1.1,"R":2.7,"C":3.7,"dC":0.6,"FT":5.9,"dF":1,"FE":6.1,"QF":7.8,"X":0.8,"H":1.3,"G":1.1,"L":1.8,"ET":2.4,"EE":2.9,"IV":2.9}
-DUM = {"in": 0, "ft": 0, "et": 0, "sk": (2, 1)}
-FLOPS = 2 * 2 * (B * 512) * D * D + 2 * B * 512 * 512 * D
+LAST = 2 * ITERS - 2
+FLOPS = 2 * 2 * (B * D) * D * D + 2 * B * D * D * D
+
+CHAIN_0 = 7
+CHAIN_EVERY = NT
+ADD_AT = 1
+SQUARE_AT = 3
+NORM_AT = 7
+SCALE_AT = 9
+TURN_AT = 12
+TURN_COPY_AT = 13
+PACK_AT = 16
+COS_AT = 17
+EXP_AT = 18
+HIGH_AT = 19
+LOW_AT = 20
+ET_AT = 21
+ET_COPY_AT = 22
+FIRST_A_AT = 22
+FIRST_MATVEC_AT = 29
+FIRST_CHAIN_AT = 33
+BIAS_AT = 3
+FRONT_ROUNDS = CHAIN_0 + 3 * CHAIN_EVERY + ET_COPY_AT + NT
 
 
 def tile_sinkhornot_kernel(tc, drone_tokens, sat_tokens, Wq, bq, Wk, bk, out_0, out_1):
@@ -43,13 +49,13 @@ def tile_sinkhornot_kernel(tc, drone_tokens, sat_tokens, Wq, bq, Wk, bk, out_0, 
         const = ctx.enter_context(tc.tile_pool(name="const", bufs=1))
         keep = ctx.enter_context(tc.tile_pool(name="keep", bufs=1))
         grp = ctx.enter_context(tc.tile_pool(name="grp", bufs=4))
-        ypool = ctx.enter_context(tc.tile_pool(name="ypool", bufs=16))
-        qpool = ctx.enter_context(tc.tile_pool(name="qpool", bufs=16))
+        ypool = ctx.enter_context(tc.tile_pool(name="ypool", bufs=4 * NT))
+        qpool = ctx.enter_context(tc.tile_pool(name="qpool", bufs=4 * NT))
         junk = ctx.enter_context(tc.tile_pool(name="junk", bufs=2))
         vec = ctx.enter_context(tc.tile_pool(name="vec", bufs=3))
-        outp = ctx.enter_context(tc.tile_pool(name="outp", bufs=8))
-        ps_f = ctx.enter_context(tc.psum_pool(name="ps_f", bufs=NF))
-        ps_b = ctx.enter_context(tc.psum_pool(name="ps_b", bufs=8 - NF))
+        outp = ctx.enter_context(tc.tile_pool(name="outp", bufs=B * NT))
+        ps_f = ctx.enter_context(tc.psum_pool(name="ps_f", bufs=6))
+        ps_b = ctx.enter_context(tc.psum_pool(name="ps_b", bufs=2))
 
         def copy_on(eng, out, in_):
             if eng == "V":
@@ -64,9 +70,9 @@ def tile_sinkhornot_kernel(tc, drone_tokens, sat_tokens, Wq, bq, Wk, bk, out_0, 
             brows.append(brow)
 
         def load(name, view):
-            raw = keep.tile([P, NT * D], BF16, name=name)
-            nc.sync.dma_start(out=raw[:].rearrange("p (n k) -> p n k", n=NT), in_=view)
-            return raw
+            dst = keep.tile([P, NT * D], BF16, name=name)
+            nc.sync.dma_start(out=dst[:].rearrange("p (n k) -> p n k", n=NT), in_=view)
+            return dst
 
         raw = {}
         raw["wq"] = load("raw_wq", Wq.rearrange("(p n) k -> p n k", n=NT))
@@ -84,8 +90,8 @@ def tile_sinkhornot_kernel(tc, drone_tokens, sat_tokens, Wq, bq, Wk, bk, out_0, 
         make_identity(nc, ident_b[:])
         ones_b = const.tile([P, P], BF16, name="ones_b")
         nc.vector.memset(ones_b[:], 1.0)
-        negh_f = const.tile([P, P], F32, name="negh_f")
-        nc.vector.memset(negh_f[:], -1.0 / B)
+        minus_mean = const.tile([P, P], F32, name="minus_mean")
+        nc.vector.memset(minus_mean[:], -1.0 / B)
         neg10 = const.tile([P, 1], F32, name="neg10")
         nc.vector.memset(neg10[:], -10.0)
         mhalf = const.tile([P, NT], F32, name="mhalf")
@@ -100,7 +106,7 @@ def tile_sinkhornot_kernel(tc, drone_tokens, sat_tokens, Wq, bq, Wk, bk, out_0, 
             nc.tensor.matmul(out=ps[:], lhsT=ones_b[:], rhs=brows[i][:], start=True, stop=True)
             bias_sb = const.tile([P, D], F32, name="bias%d" % i)
             copy_on(
-                BIAS_ENG[i],
+                "SV"[i],
                 bias_sb[:].rearrange("p (n q) -> p n q", n=NT),
                 ps[:].rearrange("p (q n) -> p n q", n=NT),
             )
@@ -111,28 +117,39 @@ def tile_sinkhornot_kernel(tc, drone_tokens, sat_tokens, Wq, bq, Wk, bk, out_0, 
         bank = {}
 
         def mx_tiles(name):
-            c = keep.tile([P, D], U32, name="c_" + name, align_bytes=64)
-            s = keep.tile([P, D], U8, name="s_" + name, align_bytes=64)
-            codes[name] = (c, s)
+            words = keep.tile([P, D], U32, name="c_" + name, align_bytes=64)
+            scales = keep.tile([P, D], U8, name="s_" + name, align_bytes=64)
+            codes[name] = (words, scales)
+            side_by_side = grp.tile([P, NT * P * 4], BF16, tag="grouped", align_bytes=64)
+            grouped[name] = side_by_side
 
         def quantise(name):
-            c, s = codes[name]
-            nc.vector.quantize_mx(out=c[:].bitcast(FP8X4), scales=s[:], in_=grouped[name][:])
+            words, scales = codes[name]
+            nc.vector.quantize_mx(out=words[:].bitcast(FP8X4), scales=scales[:], in_=grouped[name][:])
 
-        def in_T(x, h):
+        def mx_pass(out, stationary, n, moving):
+            nc.tensor.matmul_mx(
+                out=out,
+                lhsT=codes[stationary][0][:, n * P:(n + 1) * P].bitcast(FP8X4),
+                lhsT_scale=codes[stationary][1][:, n * P:(n + 1) * P],
+                rhs=codes[moving][0][:].bitcast(FP8X4),
+                rhs_scale=codes[moving][1][:],
+                start=True,
+                stop=True,
+            )
+
+        def in_turn(x, h):
             if h == 0:
                 mx_tiles(x)
-                g = grp.tile([P, NT * P * 4], BF16, tag="grouped", align_bytes=64)
-                grouped[x] = g
-            words = raw[x][:].bitcast(F32)
+            pairs = raw[x][:].bitcast(F32)
             xt = ps_f.tile([P, 2, 2, P], F32, tag="f")
             for r in range(2):
                 for u in range(2):
                     col = (2 * h + r) * 256 + u * P
-                    nc.tensor.transpose(xt[:, r, u, :], words[:, col:col + P], ident_f[:])
+                    nc.tensor.transpose(xt[:, r, u, :], pairs[:, col:col + P], ident_f[:])
             bank[(x, h)] = xt
 
-        def in_E(x, h, eng):
+        def in_copy(x, h, eng):
             gw = grouped[x][:].bitcast(F32).rearrange("p (h r w u) -> p h r w u", h=2, r=2, w=P, u=2)
             copy_on(eng, gw[:, h], bank[(x, h)][:].rearrange("p r u w -> p r w u"))
 
@@ -141,88 +158,63 @@ def tile_sinkhornot_kernel(tc, drone_tokens, sat_tokens, Wq, bq, Wk, bk, out_0, 
         ss = {}
         rn = {}
 
-        def pr_M(c, w, n):
+        def project(c, w, n):
             z = ps_f.tile([P, D], F32, tag="f")
-            nc.tensor.matmul_mx(
-                out=z[:],
-                lhsT=codes[c][0][:, n * P:(n + 1) * P].bitcast(FP8X4),
-                lhsT_scale=codes[c][1][:, n * P:(n + 1) * P],
-                rhs=codes[w][0][:].bitcast(FP8X4),
-                rhs_scale=codes[w][1][:],
-                start=True,
-                stop=True,
-            )
+            mx_pass(z[:], c, n, w)
             bank[(c, "z", n)] = z
 
-        def pr_A(c, bi, n):
+        def add_bias(c, i, n):
             y = ypool.tile([P, D], F32, tag="y")
-            nc.vector.tensor_tensor(out=y[:], in0=bank[(c, "z", n)][:], in1=bias[bi][:], op=ALU.add)
+            nc.vector.tensor_tensor(out=y[:], in0=bank[(c, "z", n)][:], in1=bias[i][:], op=ALU.add)
             ys[(c, n)] = y
 
-        def pr_S(c, n):
+        def square(c, n):
             if n == 0:
                 ss[c] = keep.tile([P, NT], F32, name="ss" + c)
             sq = junk.tile([P, D], BF16, tag="sq")
             nc.scalar.activation(out=sq[:], in_=ys[(c, n)][:], func=ACT.Square, accum_out=ss[c][:, n:n + 1])
 
-        def pr_R(c):
+        def inverse_norm(c):
             rn[c] = keep.tile([P, NT], F32, name="rn" + c)
             ssc = keep.tile([P, NT], F32, name="ssc" + c)
             nc.gpsimd.tensor_scalar(out=ssc[:], in0=ss[c][:], scalar1=1e-24, scalar2=0.0, op0=ALU.max, op1=ALU.add)
             nc.gpsimd.tensor_tensor(out=rn[c][:], in0=ssc[:], in1=mhalf[:], op=ALU.pow)
 
-        def pr_C(c, n, eng):
+        def scale(c, n):
             qb = qpool.tile([P, D], BF16, tag="qb")
-            if eng == "G":
+            if n % 2 == 0:
                 nc.gpsimd.tensor_scalar(
-                    out=qb[:], in0=ys[(c, n)][:], scalar1=rn[c][:, n:n + 1], scalar2=0.0, op0=ALU.mult, op1=ALU.add
-                )
-            elif eng == "V":
-                nc.vector.tensor_scalar(
                     out=qb[:], in0=ys[(c, n)][:], scalar1=rn[c][:, n:n + 1], scalar2=0.0, op0=ALU.mult, op1=ALU.add
                 )
             else:
                 nc.scalar.activation(out=qb[:], in_=ys[(c, n)][:], func=ACT.Copy, scale=rn[c][:, n:n + 1])
             qbs[(c, n)] = qb
 
-        def ft_T(c, h):
+        def turn(c, h):
             if h == 0:
                 mx_tiles("n" + c)
-                g = grp.tile([P, NT * P * 4], BF16, tag="grouped", align_bytes=64)
-                grouped["n" + c] = g
             qt = ps_b.tile([P, 2, NT, P], BF16, tag="b")
             for r in range(2):
                 for t in range(NT):
                     nc.tensor.transpose(qt[:, r, t, :], qbs[(c, 2 * h + r)][:, t * P:(t + 1) * P], ident_b[:])
             bank[(c, "qt", h)] = qt
 
-        def ft_E(c, h, eng):
+        def turn_copy(c, h):
             gv = grouped["n" + c][:].rearrange("p (h r w t) -> p h r w t", h=2, r=2, w=P, t=4)
-            copy_on(eng, gv[:, h], bank[(c, "qt", h)][:].rearrange("p r t w -> p r w t"))
+            copy_on("SV"[h], gv[:, h], bank[(c, "qt", h)][:].rearrange("p r t w -> p r w t"))
 
         E = {}
-        GC = {}
         KH = {}
         KL = {}
         KT = {}
         r1 = {}
 
-        def cs_M(b, n):
+        def cosine(b, n):
             z = ps_f.tile([P, D], F32, tag="f")
-            cq = codes["nd%d" % b]
-            ck = codes["ns%d" % b]
-            nc.tensor.matmul_mx(
-                out=z[:],
-                lhsT=cq[0][:, n * P:(n + 1) * P].bitcast(FP8X4),
-                lhsT_scale=cq[1][:, n * P:(n + 1) * P],
-                rhs=ck[0][:].bitcast(FP8X4),
-                rhs_scale=ck[1][:],
-                start=True,
-                stop=True,
-            )
+            mx_pass(z[:], "nd%d" % b, n, "ns%d" % b)
             bank[(b, "c", n)] = z
 
-        def cs_X(b, n):
+        def exponential(b, n):
             if n == 0:
                 r1[b] = keep.tile([P, NT], F32, name="r1_%d" % b)
             e = keep.tile([P, D], F32, name="e%d_%d" % (b, n))
@@ -232,7 +224,33 @@ def tile_sinkhornot_kernel(tc, drone_tokens, sat_tokens, Wq, bq, Wk, bk, out_0, 
             )
             E[(b, n)] = e
 
-        def cs_G(b, n, half):
+        def high_part(b, n):
+            kh = keep.tile([P, D], BF16, name="kh%d_%d" % (b, n))
+            nc.vector.tensor_copy(out=kh[:], in_=E[(b, n)][:])
+            KH[(b, n)] = kh
+
+        def low_part(b, n):
+            kl = keep.tile([P, D], BF16, name="kl%d_%d" % (b, n))
+            nc.vector.tensor_tensor(out=kl[:], in0=E[(b, n)][:], in1=KH[(b, n)][:], op=ALU.subtract)
+            KL[(b, n)] = kl
+
+        def et_turn(b, n):
+            if n == 0:
+                KT[b] = keep.tile([P, NT, 2, NT, P], BF16, name="kt%d" % b)
+            kt_ps = ps_f.tile([P, 2, NT, P], BF16, tag="f")
+            for part, src in enumerate((KH, KL)):
+                for m in range(NT):
+                    nc.tensor.transpose(kt_ps[:, part, m, :], src[(b, n)][:, m * P:(m + 1) * P], ident_b[:])
+            bank[(b, "kt", n)] = kt_ps
+
+        def et_copy(b, n):
+            nc.scalar.copy(out=KT[b][:, :, :, n, :], in_=bank[(b, "kt", n)][:].rearrange("p part m i -> p m part i"))
+
+        GC = {}
+        GH = {}
+        GL = {}
+
+        def g_make(b, n, half):
             if half == 0:
                 GC[(b, n)] = keep.tile([P, D], F32, name="g%d_%d" % (b, n))
             cols = slice(half * (D // 2), (half + 1) * (D // 2))
@@ -241,31 +259,12 @@ def tile_sinkhornot_kernel(tc, drone_tokens, sat_tokens, Wq, bq, Wk, bk, out_0, 
                 op0=ALU.add, op1=ALU.mult,
             )
 
-        def cs_H(b, n, eng):
-            kh = keep.tile([P, D], BF16, name="kh%d_%d" % (b, n))
-            if eng == "G":
-                nc.gpsimd.tensor_scalar(out=kh[:], in0=E[(b, n)][:], scalar1=1.0, scalar2=0.0, op0=ALU.mult, op1=ALU.add)
-            else:
-                copy_on(eng, kh[:], E[(b, n)][:])
-            KH[(b, n)] = kh
-
-        def cs_L(b, n, eng):
-            kl = keep.tile([P, D], BF16, name="kl%d_%d" % (b, n))
-            if eng == "V":
-                nc.vector.tensor_tensor(out=kl[:], in0=E[(b, n)][:], in1=KH[(b, n)][:], op=ALU.subtract)
-            else:
-                nc.gpsimd.tensor_tensor(out=kl[:], in0=E[(b, n)][:], in1=KH[(b, n)][:], op=ALU.subtract)
-            KL[(b, n)] = kl
-
-        GH = {}
-        GL = {}
-
-        def g_H(b, n):
+        def g_high(b, n):
             gh = keep.tile([P, D], BF16, name="gh%d_%d" % (b, n))
             nc.scalar.copy(out=gh[:], in_=GC[(b, n)][:])
             GH[(b, n)] = gh
 
-        def g_L(b, n, half):
+        def g_low(b, n, half):
             if half == 0:
                 GL[(b, n)] = keep.tile([P, D], BF16, name="gl%d_%d" % (b, n))
             cols = slice(half * (D // 2), (half + 1) * (D // 2))
@@ -273,195 +272,167 @@ def tile_sinkhornot_kernel(tc, drone_tokens, sat_tokens, Wq, bq, Wk, bk, out_0, 
                 out=GL[(b, n)][:, cols], in0=GC[(b, n)][:, cols], in1=GH[(b, n)][:, cols], op=ALU.subtract
             )
 
-        def et_T(b, n):
-            if n == 0:
-                KT[b] = keep.tile([P, NT, 2, NT, P], BF16, name="kt%d" % b)
-            kt_ps = ps_b.tile([P, 2, NT, P], BF16, tag="b")
-            for s, src in enumerate((KH, KL)):
-                for m in range(NT):
-                    nc.tensor.transpose(kt_ps[:, s, m, :], src[(b, n)][:, m * P:(m + 1) * P], ident_b[:])
-            bank[(b, "kt", n)] = kt_ps
+        vecs = {}
+        accs = {}
+        bbs = {}
+        otp = keep.tile([P, B], F32, name="otp")
 
-        def et_E(b, n, eng):
-            copy_on(eng, KT[b][:, :, :, n, :], bank[(b, "kt", n)][:].rearrange("p s m i -> p m s i"))
-
-        def dummy(k, name):
-            for i_ in range(k):
-                jz = ps_f.tile([P, D], F32, tag="f")
-                cw = codes[name]
-                nc.tensor.matmul_mx(
-                    out=jz[:], lhsT=cw[0][:, 0:P].bitcast(FP8X4), lhsT_scale=cw[1][:, 0:P],
-                    rhs=cw[0][:].bitcast(FP8X4), rhs_scale=cw[1][:], start=True, stop=True,
-                )
-
-        fillers = []
-
-        taken = [0]
-
-        def fill(k=1):
-            for i_ in range(k):
-                while taken[0] < len(fillers):
-                    on_vector, fn, args = fillers[taken[0]]
-                    taken[0] += 1
-                    fn(*args)
-                    if on_vector:
-                        break
-
-        def invert(s, b, split=True, filled=True):
-            v = vec.tile([P, NT], F32, tag="v%d" % b)
-            nc.vector.reciprocal(out=v[:], in_=s)
-            if not split:
-                return v, None
-            hl = vec.tile([P, NT, 2], BF16, tag="hl%d" % b)
-            with nc.allow_low_precision(reason="high half of a two-term bfloat16 split; the low half takes up the rest"):
-                nc.vector.reciprocal(out=hl[:, :, 0], in_=s)
-            if filled:
-                fill(FILL[1])
-            nc.vector.tensor_tensor(out=hl[:, :, 1], in0=v[:], in1=hl[:, :, 0], op=ALU.subtract)
-            if filled:
-                fill(FILL[2])
-            return v, hl
-
-        def matvec(b, stationary, hl):
+        def matvec(parts, hl):
             acc = ps_f.tile([P, NT, 2], F32, tag="f")
             for m in range(NT):
-                for c in range(NT):
-                    for s in range(2):
+                for k in range(NT):
+                    for part in range(2):
                         nc.tensor.matmul(
                             out=acc[:, m, :],
-                            lhsT=stationary(s, c, m),
-                            rhs=hl[:, c, :],
-                            start=(c == 0 and s == 0),
-                            stop=(c == NT - 1 and s == 1),
+                            lhsT=parts(part, k, m),
+                            rhs=hl[:, k, :],
+                            start=(k == 0 and part == 0),
+                            stop=(k == NT - 1 and part == 1),
                         )
             return acc
-
-        def chain(b, acc, split=True):
-            tot = vec.tile([P, NT], F32, tag="tot%d" % b)
-            nc.vector.tensor_reduce(out=tot[:], in_=acc[:], axis=AX.X, op=ALU.add)
-            fill(FILL[0])
-            return invert(tot[:], b, split)
-
-        def col_stat(b):
-            return lambda s, c, m: (KH, KL)[s][(b, c)][:, m * P:(m + 1) * P]
-
-        def row_stat(b):
-            return lambda s, c, m: KT[b][:, c, s, m, :]
-
-        plan_ = []
-
-        def at(t, fn, *args):
-            plan_.append((t, len(plan_), fn, args))
-
-        ARR = {"wq": 2.9, "d0": 3.9, "wk": 4.9, "s0": 5.9, "d1": 6.9, "s1": 7.9}
-        for x in ARR:
-            for h in range(2):
-                at(ARR[x] + 0.3 * h, in_T, x, h)
-                at(ARR[x] + 0.7 + 0.1 * h, in_E, x, h, IE_ENG[x][h])
-            at(ARR[x] + QI_OFF, quantise, x)
-            if x not in ("wq", "d0"):
-                at(ARR[x] + 0.35, dummy, DUM["in"], "wq")
-        at(BIAS_T, bias_tile, 0)
-        at(BIAS_T + 0.1, bias_tile, 1)
-        chains = ("d0", "s0", "d1", "s1")
-        wof = {"d0": "wq", "s0": "wk", "d1": "wq", "s1": "wk"}
-        bof = {"d0": 0, "s0": 1, "d1": 0, "s1": 1}
-        for i, c in enumerate(chains):
-            t0 = CH[i]
-            for n in range(NT):
-                at(t0 + 0.25 * n, pr_M, c, wof[c], n)
-                at(t0 + OFF["A"] + 0.45 * n, pr_A, c, bof[c], n)
-                at(t0 + OFF["S"] + 0.45 * n, pr_S, c, n)
-            at(t0 + OFF["R"], pr_R, c)
-            for n in range(NT):
-                at(t0 + OFF["C"] + OFF["dC"] * n, pr_C, c, n, SCALE_ENG[i][n])
-            for h in range(2):
-                at(t0 + OFF["FT"] + OFF["dF"] * h, ft_T, c, h)
-                at(t0 + OFF["FE"] + OFF["dF"] * h, ft_E, c, h, FE_ENG[i][h])
-                at(t0 + OFF["FT"] + OFF["dF"] * h + 0.01, dummy, DUM["ft"], "wq")
-            at(t0 + OFF["QF"], quantise, "n" + c)
-        for b in range(B):
-            t2 = CS[b]
-            for n in range(NT):
-                at(t2 + 0.25 * n, cs_M, b, n)
-                at(t2 + OFF["X"] + 0.5 * n, cs_X, b, n)
-                at(t2 + OFF["H"] + 0.5 * n, cs_H, b, n, H_ENG[b][n])
-                at(t2 + OFF["L"] + 0.5 * n, cs_L, b, n, L_ENG[b][n])
-                at(t2 + OFF["ET"] + 0.5 * n, et_T, b, n)
-                at(t2 + OFF["EE"] + 0.5 * n, et_E, b, n, EE_ENG[b][n])
-                at(t2 + OFF["ET"] + 0.5 * n + 0.01, dummy, DUM["et"], "wq")
-        av = [None, None]
-        bv = [None, None]
-
-        def first_a(b):
-            av[b] = invert(r1[b][:], b, True, False)
-
-        for b in range(B):
-            at(CS[b] + OFF["IV"], first_a, b)
-        for t, i, fn, args in sorted(plan_):
-            fn(*args)
-
-        tiles = [(b, n) for b in range(B) for n in range(NT)]
-        for i in range(len(tiles) + LAG):
-            if i < len(tiles):
-                b, n = tiles[i]
-                fillers.append((False, cs_M, (b, n)))
-                fillers.append((True, cs_G, (b, n, 0)))
-                fillers.append((True, cs_G, (b, n, 1)))
-                fillers.append((False, g_H, (b, n)))
-            if i >= LAG:
-                b, n = tiles[i - LAG]
-                fillers.append((True, g_L, (b, n, 0)))
-                fillers.append((True, g_L, (b, n, 1)))
-
-        for it in range(ITERS):
-            if it > 0:
-                for b in range(B):
-                    acc = matvec(b, row_stat(b), bv[b][1])
-                    dummy(DUM["sk"][b], "wq")
-                    av[b] = chain(b, acc)
-            for b in range(B):
-                acc = matvec(b, col_stat(b), av[b][1])
-                dummy(DUM["sk"][b], "wq")
-                bv[b] = chain(b, acc, it < ITERS - 1)
-        fill(len(fillers))
-
-        otp = keep.tile([P, B], F32, name="otp")
-        bbs = []
-        waccs = []
-        for b in range(B):
-            bb = ps_f.tile([P, D], F32, tag="f")
-            for m in range(NT):
-                nc.tensor.transpose(
-                    bb[:, m * P:(m + 1) * P], bv[b][0][:, m:m + 1].to_broadcast([P, P]), ident_f[:]
-                )
-            bbs.append(bb)
-        for b in range(B):
-            waccs.append(matvec(b, lambda s, c, m, b=b: (GH, GL)[s][(b, c)][:, m * P:(m + 1) * P], av[b][1]))
 
         def plan_tile(b, n):
             plan = outp.tile([P, D], F32, tag="plan")
             nc.vector.scalar_tensor_tensor(
-                out=plan[:], in0=E[(b, n)][:], scalar=av[b][0][:, n:n + 1], in1=bbs[b][:], op0=ALU.mult, op1=ALU.mult
+                out=plan[:], in0=E[(b, n)][:], scalar=vecs[(b, LAST - 1)][0][:, n:n + 1], in1=bbs[b][:],
+                op0=ALU.mult, op1=ALU.mult,
             )
             nc.sync.dma_start(out=out_0[b].rearrange("(p n) j -> p n j", n=NT)[:, n, :], in_=plan[:])
+
+        def end_tensor(b):
+            bb = ps_f.tile([P, D], F32, tag="f")
+            for m in range(NT):
+                nc.tensor.transpose(
+                    bb[:, m * P:(m + 1) * P], vecs[(b, LAST)][0][:, m:m + 1].to_broadcast([P, P]), ident_f[:]
+                )
+            bbs[b] = bb
+            accs[(b, "w")] = matvec(lambda part, k, m: (GH, GL)[part][(b, k)][:, m * P:(m + 1) * P], vecs[(b, LAST - 1)][1])
 
         def ot_part(b):
             wj = vec.tile([P, NT, 2], F32, tag="wj")
             nc.vector.scalar_tensor_tensor(
-                out=wj[:], in0=waccs[b][:], scalar=1.0, in1=bv[b][0][:].unsqueeze(2).to_broadcast([P, NT, 2]),
+                out=wj[:], in0=accs[(b, "w")][:], scalar=1.0,
+                in1=vecs[(b, LAST)][0][:].unsqueeze(2).to_broadcast([P, NT, 2]),
                 op0=ALU.mult, op1=ALU.mult, accum_out=otp[:, b:b + 1],
             )
 
-        for n in range(NT):
-            plan_tile(0, n)
+        def side_work(b, s, half):
+            if s < NT:
+                g_make(b, s, half)
+            elif s < 2 * NT:
+                g_low(b, s - NT, half)
+            elif b == 1:
+                plan_tile(0, half)
+
+        def invert(b, s, tot):
+            full = vec.tile([P, NT], F32, tag="v%d" % b)
+            nc.vector.reciprocal(out=full[:], in_=tot)
+            hl = None
+            if s < LAST:
+                hl = vec.tile([P, NT, 2], BF16, tag="hl%d" % b)
+                with nc.allow_low_precision(reason="high half of a two-term bfloat16 split; the low half takes up the rest"):
+                    nc.vector.reciprocal(out=hl[:, :, 0], in_=tot)
+            vecs[(b, s)] = (full, hl)
+
+        def split(b, s):
+            full, hl = vecs[(b, s)]
+            nc.vector.tensor_tensor(out=hl[:, :, 1], in0=full[:], in1=hl[:, :, 0], op=ALU.subtract)
+
+        def step_tensor(b, s):
+            if s % 2 == 0:
+                accs[(b, s)] = matvec(lambda part, k, m: (KH, KL)[part][(b, k)][:, m * P:(m + 1) * P], vecs[(b, s - 1)][1])
+            else:
+                accs[(b, s)] = matvec(lambda part, k, m: KT[b][:, k, part, m, :], vecs[(b, s - 1)][1])
+            if s < NT:
+                cosine(b, s)
+
+        def step_vector(b, s):
+            tot = vec.tile([P, NT], F32, tag="tot%d" % b)
+            nc.vector.tensor_reduce(out=tot[:], in_=accs[(b, s)][:], axis=AX.X, op=ALU.add)
+            side_work(b, s, 0)
+            invert(b, s, tot[:])
+            side_work(b, s, 1)
+            if s < LAST:
+                split(b, s)
+            if s < NT:
+                g_high(b, s)
+
+        inputs = ("wq", "d0", "wk", "s0", "d1", "s1")
+        chains = ("d0", "s0", "d1", "s1")
+        for rnd in range(FRONT_ROUNDS):
+            for i, c in enumerate(chains):
+                at = rnd - (CHAIN_0 + CHAIN_EVERY * i)
+                b = i // 2
+                if i % 2 == 1:
+                    if at == FIRST_CHAIN_AT and b == 0:
+                        step_vector(b, 0)
+                    if at == FIRST_MATVEC_AT and b == 0:
+                        step_tensor(b, 0)
+                    if at == FIRST_A_AT:
+                        invert(b, -1, r1[b][:])
+                    if at == FIRST_A_AT + 1:
+                        split(b, -1)
+                    if 0 <= at - ET_COPY_AT < NT:
+                        et_copy(b, at - ET_COPY_AT)
+                    if 0 <= at - ET_AT < NT:
+                        et_turn(b, at - ET_AT)
+                    if 0 <= at - LOW_AT < NT:
+                        low_part(b, at - LOW_AT)
+                    if 0 <= at - HIGH_AT < NT:
+                        high_part(b, at - HIGH_AT)
+                    if 0 <= at - EXP_AT < NT:
+                        exponential(b, at - EXP_AT)
+                    if 0 <= at - COS_AT < NT:
+                        cosine(b, at - COS_AT)
+                if at == PACK_AT:
+                    quantise("n" + c)
+                for h in range(2):
+                    if at == TURN_COPY_AT + 2 * h:
+                        turn_copy(c, h)
+                    if at == TURN_AT + 2 * h:
+                        turn(c, h)
+                if 0 <= at - SCALE_AT < NT:
+                    scale(c, at - SCALE_AT)
+                if at == NORM_AT:
+                    inverse_norm(c)
+                if 0 <= at - SQUARE_AT < NT:
+                    square(c, at - SQUARE_AT)
+                if 0 <= at - ADD_AT < NT:
+                    add_bias(c, i % 2, at - ADD_AT)
+                if 0 <= at < NT:
+                    project(c, ("wq", "wk")[i % 2], at)
+            for j, x in enumerate(inputs):
+                at = rnd - 2 * j
+                if at == 4:
+                    quantise(x)
+                for h in range(2):
+                    if at == 2 + h:
+                        in_copy(x, h, "V" if (h == 1 and j < 2) else "S")
+                    if at == h:
+                        in_turn(x, h)
+            if rnd == BIAS_AT:
+                bias_tile(0)
+                bias_tile(1)
+
+        for s in range(LAST + 1):
+            step_tensor(1, s)
+            if s < LAST:
+                step_tensor(0, s + 1)
+            else:
+                end_tensor(0)
+            step_vector(1, s)
+            if s < LAST:
+                step_vector(0, s + 1)
+        end_tensor(1)
+        plan_tile(0, 2)
+        plan_tile(0, 3)
         ot_part(0)
         plan_tile(1, 0)
         plan_tile(1, 1)
         ot_part(1)
         fin = ps_f.tile([P, 1], F32, tag="f")
         for b in range(B):
-            nc.tensor.matmul(out=fin[:], lhsT=negh_f[:], rhs=otp[:, b:b + 1], start=(b == 0), stop=(b == B - 1))
+            nc.tensor.matmul(out=fin[:], lhsT=minus_mean[:], rhs=otp[:, b:b + 1], start=(b == 0), stop=(b == B - 1))
         plan_tile(1, 2)
         res = keep.tile([P, 1], F32, name="res")
         nc.vector.tensor_copy(out=res[:], in_=fin[:])

from contextlib import ExitStack

import concourse.mybir as mybir
from concourse.masks import make_identity

F32 = mybir.dt.float32
BF16 = mybir.dt.bfloat16
U32 = mybir.dt.uint32
U8 = mybir.dt.uint8
FP8X4 = mybir.dt.float8_e4m3fn_x4
ACT = mybir.ActivationFunctionType
ALU = mybir.AluOpType
AX = mybir.AxisListType

P = 128
D = 512
NT = D // P
B = 2
ITERS = 5
LAST = 2 * ITERS - 2
FLOPS = 2 * 2 * (B * D) * D * D + 2 * B * D * D * D

CHAIN_0 = 7
CHAIN_EVERY = NT
ADD_AT = 1
SQUARE_AT = 3
NORM_AT = 7
SCALE_AT = 9
TURN_AT = 12
TURN_COPY_AT = 13
PACK_AT = 16
COS_AT = 17
EXP_AT = 18
HIGH_AT = 19
LOW_AT = 20
ET_AT = 21
ET_COPY_AT = 22
FIRST_A_AT = 22
FIRST_MATVEC_AT = 29
FIRST_CHAIN_AT = 33
BIAS_AT = 3
FRONT_ROUNDS = CHAIN_0 + 3 * CHAIN_EVERY + ET_COPY_AT + NT


def tile_sinkhornot_kernel(tc, drone_tokens, sat_tokens, Wq, bq, Wk, bk, out_0, out_1):
    nc = tc.nc
    with ExitStack() as ctx:
        ctx.enter_context(tc.manual_schedule())
        const = ctx.enter_context(tc.tile_pool(name="const", bufs=1))
        keep = ctx.enter_context(tc.tile_pool(name="keep", bufs=1))
        grp = ctx.enter_context(tc.tile_pool(name="grp", bufs=4))
        ypool = ctx.enter_context(tc.tile_pool(name="ypool", bufs=4 * NT))
        qpool = ctx.enter_context(tc.tile_pool(name="qpool", bufs=4 * NT))
        junk = ctx.enter_context(tc.tile_pool(name="junk", bufs=2))
        vec = ctx.enter_context(tc.tile_pool(name="vec", bufs=3))
        outp = ctx.enter_context(tc.tile_pool(name="outp", bufs=B * NT))
        ps_f = ctx.enter_context(tc.psum_pool(name="ps_f", bufs=6))
        ps_b = ctx.enter_context(tc.psum_pool(name="ps_b", bufs=2))

        def copy_on(eng, out, in_):
            if eng == "V":
                nc.vector.tensor_copy(out=out, in_=in_)
            else:
                nc.scalar.copy(out=out, in_=in_)

        brows = []
        for i in range(2):
            brow = const.tile([P, D], BF16, name="brow%d" % i)
            nc.vector.memset(brow[:], 0.0)
            brows.append(brow)

        def load(name, view):
            dst = keep.tile([P, NT * D], BF16, name=name)
            nc.sync.dma_start(out=dst[:].rearrange("p (n k) -> p n k", n=NT), in_=view)
            return dst

        raw = {}
        raw["wq"] = load("raw_wq", Wq.rearrange("(p n) k -> p n k", n=NT))
        raw["d0"] = load("raw_d0", drone_tokens[0].rearrange("(p n) k -> p n k", n=NT))
        for i, bvec in enumerate((bq, bk)):
            nc.sync.dma_start(out=brows[i][0:1, :], in_=bvec.rearrange("(o f) -> o f", o=1))
        raw["wk"] = load("raw_wk", Wk.rearrange("(p n) k -> p n k", n=NT))
        raw["s0"] = load("raw_s0", sat_tokens[0].rearrange("(n p) k -> p n k", p=P))
        raw["d1"] = load("raw_d1", drone_tokens[1].rearrange("(p n) k -> p n k", n=NT))
        raw["s1"] = load("raw_s1", sat_tokens[1].rearrange("(n p) k -> p n k", p=P))

        ident_f = const.tile([P, P], F32, name="ident_f")
        make_identity(nc, ident_f[:])
        ident_b = const.tile([P, P], BF16, name="ident_b")
        make_identity(nc, ident_b[:])
        ones_b = const.tile([P, P], BF16, name="ones_b")
        nc.vector.memset(ones_b[:], 1.0)
        minus_mean = const.tile([P, P], F32, name="minus_mean")
        nc.vector.memset(minus_mean[:], -1.0 / B)
        neg10 = const.tile([P, 1], F32, name="neg10")
        nc.vector.memset(neg10[:], -10.0)
        mhalf = const.tile([P, NT], F32, name="mhalf")
        nc.vector.memset(mhalf[:], -0.5)
        warm = const.tile([P, 1], F32, name="warm")
        nc.scalar.activation(out=warm[:], in_=neg10[:], func=ACT.Exp)

        bias = []

        def bias_tile(i):
            ps = ps_f.tile([P, D], F32, tag="f")
            nc.tensor.matmul(out=ps[:], lhsT=ones_b[:], rhs=brows[i][:], start=True, stop=True)
            bias_sb = const.tile([P, D], F32, name="bias%d" % i)
            copy_on(
                "SV"[i],
                bias_sb[:].rearrange("p (n q) -> p n q", n=NT),
                ps[:].rearrange("p (q n) -> p n q", n=NT),
            )
            bias.append(bias_sb)

        codes = {}
        grouped = {}
        bank = {}

        def mx_tiles(name):
            words = keep.tile([P, D], U32, name="c_" + name, align_bytes=64)
            scales = keep.tile([P, D], U8, name="s_" + name, align_bytes=64)
            codes[name] = (words, scales)
            side_by_side = grp.tile([P, NT * P * 4], BF16, tag="grouped", align_bytes=64)
            grouped[name] = side_by_side

        def quantise(name):
            words, scales = codes[name]
            nc.vector.quantize_mx(out=words[:].bitcast(FP8X4), scales=scales[:], in_=grouped[name][:])

        def mx_pass(out, stationary, n, moving):
            nc.tensor.matmul_mx(
                out=out,
                lhsT=codes[stationary][0][:, n * P:(n + 1) * P].bitcast(FP8X4),
                lhsT_scale=codes[stationary][1][:, n * P:(n + 1) * P],
                rhs=codes[moving][0][:].bitcast(FP8X4),
                rhs_scale=codes[moving][1][:],
                start=True,
                stop=True,
            )

        def in_turn(x, h):
            if h == 0:
                mx_tiles(x)
            pairs = raw[x][:].bitcast(F32)
            xt = ps_f.tile([P, 2, 2, P], F32, tag="f")
            for r in range(2):
                for u in range(2):
                    col = (2 * h + r) * 256 + u * P
                    nc.tensor.transpose(xt[:, r, u, :], pairs[:, col:col + P], ident_f[:])
            bank[(x, h)] = xt

        def in_copy(x, h, eng):
            gw = grouped[x][:].bitcast(F32).rearrange("p (h r w u) -> p h r w u", h=2, r=2, w=P, u=2)
            copy_on(eng, gw[:, h], bank[(x, h)][:].rearrange("p r u w -> p r w u"))

        ys = {}
        qbs = {}
        ss = {}
        rn = {}

        def project(c, w, n):
            z = ps_f.tile([P, D], F32, tag="f")
            mx_pass(z[:], c, n, w)
            bank[(c, "z", n)] = z

        def add_bias(c, i, n):
            y = ypool.tile([P, D], F32, tag="y")
            nc.vector.tensor_tensor(out=y[:], in0=bank[(c, "z", n)][:], in1=bias[i][:], op=ALU.add)
            ys[(c, n)] = y

        def square(c, n):
            if n == 0:
                ss[c] = keep.tile([P, NT], F32, name="ss" + c)
            sq = junk.tile([P, D], BF16, tag="sq")
            nc.scalar.activation(out=sq[:], in_=ys[(c, n)][:], func=ACT.Square, accum_out=ss[c][:, n:n + 1])

        def inverse_norm(c):
            rn[c] = keep.tile([P, NT], F32, name="rn" + c)
            ssc = keep.tile([P, NT], F32, name="ssc" + c)
            nc.gpsimd.tensor_scalar(out=ssc[:], in0=ss[c][:], scalar1=1e-24, scalar2=0.0, op0=ALU.max, op1=ALU.add)
            nc.gpsimd.tensor_tensor(out=rn[c][:], in0=ssc[:], in1=mhalf[:], op=ALU.pow)

        def scale(c, n):
            qb = qpool.tile([P, D], BF16, tag="qb")
            if n % 2 == 0:
                nc.gpsimd.tensor_scalar(
                    out=qb[:], in0=ys[(c, n)][:], scalar1=rn[c][:, n:n + 1], scalar2=0.0, op0=ALU.mult, op1=ALU.add
                )
            else:
                nc.scalar.activation(out=qb[:], in_=ys[(c, n)][:], func=ACT.Copy, scale=rn[c][:, n:n + 1])
            qbs[(c, n)] = qb

        def turn(c, h):
            if h == 0:
                mx_tiles("n" + c)
            qt = ps_b.tile([P, 2, NT, P], BF16, tag="b")
            for r in range(2):
                for t in range(NT):
                    nc.tensor.transpose(qt[:, r, t, :], qbs[(c, 2 * h + r)][:, t * P:(t + 1) * P], ident_b[:])
            bank[(c, "qt", h)] = qt

        def turn_copy(c, h):
            gv = grouped["n" + c][:].rearrange("p (h r w t) -> p h r w t", h=2, r=2, w=P, t=4)
            copy_on("SV"[h], gv[:, h], bank[(c, "qt", h)][:].rearrange("p r t w -> p r w t"))

        E = {}
        KH = {}
        KL = {}
        KT = {}
        r1 = {}

        def cosine(b, n):
            z = ps_f.tile([P, D], F32, tag="f")
            mx_pass(z[:], "nd%d" % b, n, "ns%d" % b)
            bank[(b, "c", n)] = z

        def exponential(b, n):
            if n == 0:
                r1[b] = keep.tile([P, NT], F32, name="r1_%d" % b)
            e = keep.tile([P, D], F32, name="e%d_%d" % (b, n))
            nc.scalar.activation(
                out=e[:], in_=bank[(b, "c", n)][:], func=ACT.Exp, scale=10.0, bias=neg10[:],
                accum_out=r1[b][:, n:n + 1],
            )
            E[(b, n)] = e

        def high_part(b, n):
            kh = keep.tile([P, D], BF16, name="kh%d_%d" % (b, n))
            nc.vector.tensor_copy(out=kh[:], in_=E[(b, n)][:])
            KH[(b, n)] = kh

        def low_part(b, n):
            kl = keep.tile([P, D], BF16, name="kl%d_%d" % (b, n))
            nc.vector.tensor_tensor(out=kl[:], in0=E[(b, n)][:], in1=KH[(b, n)][:], op=ALU.subtract)
            KL[(b, n)] = kl

        def et_turn(b, n):
            if n == 0:
                KT[b] = keep.tile([P, NT, 2, NT, P], BF16, name="kt%d" % b)
            kt_ps = ps_f.tile([P, 2, NT, P], BF16, tag="f")
            for part, src in enumerate((KH, KL)):
                for m in range(NT):
                    nc.tensor.transpose(kt_ps[:, part, m, :], src[(b, n)][:, m * P:(m + 1) * P], ident_b[:])
            bank[(b, "kt", n)] = kt_ps

        def et_copy(b, n):
            nc.scalar.copy(out=KT[b][:, :, :, n, :], in_=bank[(b, "kt", n)][:].rearrange("p part m i -> p m part i"))

        GC = {}
        GH = {}
        GL = {}

        def g_make(b, n, half):
            if half == 0:
                GC[(b, n)] = keep.tile([P, D], F32, name="g%d_%d" % (b, n))
            cols = slice(half * (D // 2), (half + 1) * (D // 2))
            nc.vector.scalar_tensor_tensor(
                out=GC[(b, n)][:, cols], in0=bank[(b, "c", n)][:, cols], scalar=-1.0, in1=E[(b, n)][:, cols],
                op0=ALU.add, op1=ALU.mult,
            )

        def g_high(b, n):
            gh = keep.tile([P, D], BF16, name="gh%d_%d" % (b, n))
            nc.scalar.copy(out=gh[:], in_=GC[(b, n)][:])
            GH[(b, n)] = gh

        def g_low(b, n, half):
            if half == 0:
                GL[(b, n)] = keep.tile([P, D], BF16, name="gl%d_%d" % (b, n))
            cols = slice(half * (D // 2), (half + 1) * (D // 2))
            nc.vector.tensor_tensor(
                out=GL[(b, n)][:, cols], in0=GC[(b, n)][:, cols], in1=GH[(b, n)][:, cols], op=ALU.subtract
            )

        vecs = {}
        accs = {}
        bbs = {}
        otp = keep.tile([P, B], F32, name="otp")

        def matvec(parts, hl):
            acc = ps_f.tile([P, NT, 2], F32, tag="f")
            for m in range(NT):
                for k in range(NT):
                    for part in range(2):
                        nc.tensor.matmul(
                            out=acc[:, m, :],
                            lhsT=parts(part, k, m),
                            rhs=hl[:, k, :],
                            start=(k == 0 and part == 0),
                            stop=(k == NT - 1 and part == 1),
                        )
            return acc

        def plan_tile(b, n):
            plan = outp.tile([P, D], F32, tag="plan")
            nc.vector.scalar_tensor_tensor(
                out=plan[:], in0=E[(b, n)][:], scalar=vecs[(b, LAST - 1)][0][:, n:n + 1], in1=bbs[b][:],
                op0=ALU.mult, op1=ALU.mult,
            )
            nc.sync.dma_start(out=out_0[b].rearrange("(p n) j -> p n j", n=NT)[:, n, :], in_=plan[:])

        def end_tensor(b):
            bb = ps_f.tile([P, D], F32, tag="f")
            for m in range(NT):
                nc.tensor.transpose(
                    bb[:, m * P:(m + 1) * P], vecs[(b, LAST)][0][:, m:m + 1].to_broadcast([P, P]), ident_f[:]
                )
            bbs[b] = bb
            accs[(b, "w")] = matvec(lambda part, k, m: (GH, GL)[part][(b, k)][:, m * P:(m + 1) * P], vecs[(b, LAST - 1)][1])

        def ot_part(b):
            wj = vec.tile([P, NT, 2], F32, tag="wj")
            nc.vector.scalar_tensor_tensor(
                out=wj[:], in0=accs[(b, "w")][:], scalar=1.0,
                in1=vecs[(b, LAST)][0][:].unsqueeze(2).to_broadcast([P, NT, 2]),
                op0=ALU.mult, op1=ALU.mult, accum_out=otp[:, b:b + 1],
            )

        def side_work(b, s, half):
            if s < NT:
                g_make(b, s, half)
            elif s < 2 * NT:
                g_low(b, s - NT, half)
            elif b == 1:
                plan_tile(0, half)

        def invert(b, s, tot):
            full = vec.tile([P, NT], F32, tag="v%d" % b)
            nc.vector.reciprocal(out=full[:], in_=tot)
            hl = None
            if s < LAST:
                hl = vec.tile([P, NT, 2], BF16, tag="hl%d" % b)
                with nc.allow_low_precision(reason="high half of a two-term bfloat16 split; the low half takes up the rest"):
                    nc.vector.reciprocal(out=hl[:, :, 0], in_=tot)
            vecs[(b, s)] = (full, hl)

        def split(b, s):
            full, hl = vecs[(b, s)]
            nc.vector.tensor_tensor(out=hl[:, :, 1], in0=full[:], in1=hl[:, :, 0], op=ALU.subtract)

        def step_tensor(b, s):
            if s % 2 == 0:
                accs[(b, s)] = matvec(lambda part, k, m: (KH, KL)[part][(b, k)][:, m * P:(m + 1) * P], vecs[(b, s - 1)][1])
            else:
                accs[(b, s)] = matvec(lambda part, k, m: KT[b][:, k, part, m, :], vecs[(b, s - 1)][1])
            if s < NT:
                cosine(b, s)

        def step_vector(b, s):
            tot = vec.tile([P, NT], F32, tag="tot%d" % b)
            nc.vector.tensor_reduce(out=tot[:], in_=accs[(b, s)][:], axis=AX.X, op=ALU.add)
            side_work(b, s, 0)
            invert(b, s, tot[:])
            side_work(b, s, 1)
            if s < LAST:
                split(b, s)
            if s < NT:
                g_high(b, s)

        inputs = ("wq", "d0", "wk", "s0", "d1", "s1")
        chains = ("d0", "s0", "d1", "s1")
        for rnd in range(FRONT_ROUNDS):
            for i, c in enumerate(chains):
                at = rnd - (CHAIN_0 + CHAIN_EVERY * i)
                b = i // 2
                if i % 2 == 1:
                    if at == FIRST_CHAIN_AT and b == 0:
                        step_vector(b, 0)
                    if at == FIRST_MATVEC_AT and b == 0:
                        step_tensor(b, 0)
                    if at == FIRST_A_AT:
                        invert(b, -1, r1[b][:])
                    if at == FIRST_A_AT + 1:
                        split(b, -1)
                    if 0 <= at - ET_COPY_AT < NT:
                        et_copy(b, at - ET_COPY_AT)
                    if 0 <= at - ET_AT < NT:
                        et_turn(b, at - ET_AT)
                    if 0 <= at - LOW_AT < NT:
                        low_part(b, at - LOW_AT)
                    if 0 <= at - HIGH_AT < NT:
                        high_part(b, at - HIGH_AT)
                    if 0 <= at - EXP_AT < NT:
                        exponential(b, at - EXP_AT)
                    if 0 <= at - COS_AT < NT:
                        cosine(b, at - COS_AT)
                if at == PACK_AT:
                    quantise("n" + c)
                for h in range(2):
                    if at == TURN_COPY_AT + 2 * h:
                        turn_copy(c, h)
                    if at == TURN_AT + 2 * h:
                        turn(c, h)
                if 0 <= at - SCALE_AT < NT:
                    scale(c, at - SCALE_AT)
                if at == NORM_AT:
                    inverse_norm(c)
                if 0 <= at - SQUARE_AT < NT:
                    square(c, at - SQUARE_AT)
                if 0 <= at - ADD_AT < NT:
                    add_bias(c, i % 2, at - ADD_AT)
                if 0 <= at < NT:
                    project(c, ("wq", "wk")[i % 2], at)
            for j, x in enumerate(inputs):
                at = rnd - 2 * j
                if at == 4:
                    quantise(x)
                for h in range(2):
                    if at == 2 + h:
                        in_copy(x, h, "V" if (h == 1 and j < 2) else "S")
                    if at == h:
                        in_turn(x, h)
            if rnd == BIAS_AT:
                bias_tile(0)
                bias_tile(1)

        for s in range(LAST + 1):
            step_tensor(1, s)
            if s < LAST:
                step_tensor(0, s + 1)
            else:
                end_tensor(0)
            step_vector(1, s)
            if s < LAST:
                step_vector(0, s + 1)
        end_tensor(1)
        plan_tile(0, 2)
        plan_tile(0, 3)
        ot_part(0)
        plan_tile(1, 0)
        plan_tile(1, 1)
        ot_part(1)
        fin = ps_f.tile([P, 1], F32, tag="f")
        for b in range(B):
            nc.tensor.matmul(out=fin[:], lhsT=minus_mean[:], rhs=otp[:, b:b + 1], start=(b == 0), stop=(b == B - 1))
        plan_tile(1, 2)
        res = keep.tile([P, 1], F32, name="res")
        nc.vector.tensor_copy(out=res[:], in_=fin[:])
        o1 = out_1
        while len(o1.shape) < 2:
            o1 = o1.unsqueeze(0)
        nc.sync.dma_start(out=o1, in_=res[0:1, 0:1])
        plan_tile(1, 3)
